import numpy as np
import ml_dtypes


def mxq(x, axis, fmt="e4m3"):
    dtype, down = {"e4m3": (ml_dtypes.float8_e4m3fn, 7), "e5m2": (ml_dtypes.float8_e5m2, 14)}[fmt]
    v = np.moveaxis(np.asarray(x, np.float32).astype(ml_dtypes.bfloat16).astype(np.float64), axis, -1)
    blocks = v.reshape(v.shape[:-1] + (-1, 32))
    amax = np.abs(blocks).max(-1, keepdims=True)
    byte = np.maximum(np.where(amax > 0, np.frexp(amax)[1] - 1 + 127, 0) - down, 1)
    scale = np.exp2(byte - 127.0)
    codes = (blocks / scale).astype(np.float32).astype(dtype).astype(np.float64)
    return np.moveaxis((codes * scale).reshape(v.shape), -1, axis)


WIDE = False


def mx_kscale(k):
    if not WIDE:
        return np.ones(k)
    levels = np.array([10, -10, 5, -5, 0])
    a = np.random.permutation(np.resize(levels, k // 512 * 4)).reshape(k // 512, 4)
    idx = np.arange(k)
    return np.exp2(a[idx // 512, idx % 128 // 32])


BF16 = ml_dtypes.bfloat16


def bf(x):
    return np.asarray(x, np.float32).astype(BF16)


def f64(x):
    return np.asarray(x).astype(np.float64)


N, L, A, D = 8, 256, 32, 32
KP, KQ = A * D, D * D


def setup_inputs():
    u = mx_kscale(KP).reshape(A, D)[:, 0].copy()
    u[-1] = 1.0
    t = mx_kscale(KQ).reshape(D, D)[:, 0].copy()
    t[-1] = 1.0
    return {"layer1": bf(np.random.standard_normal((N, L, A - 1)) * u[:-1]),
            "layer2": bf(np.random.standard_normal((N, L, D - 1)) * 0.5 / t[:-1]),
            "layer3": bf(np.random.standard_normal((N, L, D - 1))),
            "h1": bf(np.random.standard_normal((N, L, D))),
            "h2": bf(np.random.standard_normal((N, L, D)) * 0.5),
            "h3": bf(np.random.standard_normal((N, L, D))),
            "W": bf(np.random.standard_normal((A, D, D, D)) * 0.4 / np.sqrt(KP) / u[:, None, None, None] * t[None, :, None, None])}


def reference(layer1, layer2, layer3, h1, h2, h3, W):
    n, l = layer1.shape[:2]
    ones = np.ones((n, l, 1))
    l1 = np.concatenate([f64(layer1), ones], axis=-1)
    l2 = np.concatenate([f64(layer2), ones], axis=-1)
    p = (l1[..., :, None] * f64(h1)[..., None, :]).reshape(n, l, KP)
    w = f64(W).transpose(0, 2, 1, 3).reshape(KP, KQ)
    q = mxq(p, 2, "e4m3") @ mxq(w, 0, "e4m3")
    r = (l2[..., :, None] * f64(h2)[..., None, :]).reshape(n, l, KQ)
    return mxq(q, 2, "e4m3") @ mxq(r, 2, "e4m3").transpose(0, 2, 1)

@@ -1,0 +1,202 @@
+from contextlib import ExitStack
+
+import concourse.mybir as mybir
+from concourse.masks import make_identity
+
+FLOPS = 2 * 2048 * 1024 * 1024 + 8 * 2 * 256 * 256 * 1024
+BYTES = 2 * (8 * 256 * 31 * 2) + 2 * (8 * 256 * 32 * 2) + 32 * 32 * 32 * 32 * 2 + 8 * 256 * 256 * 4
+
+BF16 = mybir.dt.bfloat16
+F32 = mybir.dt.float32
+U32 = mybir.dt.uint32
+U8 = mybir.dt.uint8
+FP8X4 = mybir.dt.float8_e4m3fn_x4
+MULT = mybir.AluOpType.mult
+
+P = 128
+NB = 8
+
+
+def tile_qriaffine_kernel(tc, layer1, layer2, layer3, h1, h2, h3, W, out):
+    nc = tc.nc
+    with ExitStack() as ctx:
+        keep = ctx.enter_context(tc.tile_pool(name="keep", bufs=1))
+        work = ctx.enter_context(tc.tile_pool(name="work", bufs=3))
+        ps_h = ctx.enter_context(tc.psum_pool(name="ps_h", bufs=2))
+        ps_l = ctx.enter_context(tc.psum_pool(name="ps_l", bufs=2))
+        ps_1 = ctx.enter_context(tc.psum_pool(name="ps_1", bufs=3))
+        ps_2 = ctx.enter_context(tc.psum_pool(name="ps_2", bufs=1))
+
+        l1r = keep.tile([P, 16 * 32], BF16, name="l1r")
+        h1r = keep.tile([P, 16 * 32], BF16, name="h1r")
+        l2r = keep.tile([P, 16 * 32], BF16, name="l2r")
+        h2r = keep.tile([P, 16 * 32], BF16, name="h2r")
+        for dst, src, width in ((l1r, layer1, 62), (h1r, h1, 64), (l2r, layer2, 62), (h2r, h2, 64)):
+            nc.scalar.dma_start(
+                out=dst[:].rearrange("p (n f) -> p n f", n=NB)[:, :, 0:width],
+                in_=src.rearrange("n (x t) a -> x n (t a)", t=2),
+            )
+        wr = [keep.tile([P, 4096], BF16, name="wr%d" % g) for g in range(2)]
+        for g in range(2):
+            for c8 in range(8):
+                nc.sync.dma_start(
+                    out=wr[g][c8:P:8, :].rearrange("p (b f) -> p b f", b=32),
+                    in_=W[16 * g : 16 * g + 16, :, 4 * c8 : 4 * c8 + 4, :].rearrange("a b j d -> a b (j d)"),
+                )
+
+        ident = keep.tile([P, P], F32, name="ident")
+        make_identity(nc, ident[:])
+
+        l1d = keep.tile([P, 1024], BF16, name="l1d")
+        l2d = keep.tile([P, 1024], BF16, name="l2d")
+        h1p = keep.tile([P, 512], BF16, name="h1p")
+        h2p = keep.tile([P, 512], BF16, name="h2p")
+        for ld, lr in ((l1d, l1r), (l2d, l2r)):
+            nc.vector.memset(ld[:], 1.0)
+            nc.vector.tensor_copy(
+                out=ld[:].rearrange("p (n t a e) -> p n t a e", t=2, a=32, e=2)[:, :, :, 0:31, :],
+                in_=lr[:]
+                .rearrange("p (n f) -> p n f", n=NB)[:, :, 0:62]
+                .rearrange("p n (t a) -> p n t a", t=2)
+                .unsqueeze(4)
+                .to_broadcast([P, NB, 2, 31, 2]),
+            )
+        for u in range(2):
+            nc.vector.tensor_copy(
+                out=h1p[:].rearrange("p (k u c e) -> p k u c e", u=2, c=8, e=2)[:, :, u, :, :],
+                in_=h1r[:].rearrange("p (k c u e) -> p k u c e", c=8, u=2, e=2)[:, :, u, :, :],
+            )
+            nc.vector.tensor_copy(
+                out=h2p[:].rearrange("p (k u d e) -> p k u d e", u=2, d=8, e=2)[:, :, u, :, :],
+                in_=h2r[:].rearrange("p (k u e d) -> p k u d e", u=2, e=2, d=8)[:, :, u, :, :],
+            )
+
+        he = [keep.tile([P, 8192], BF16, name="he%d" % s) for s in range(2)]
+        le = [keep.tile([P, 8192], BF16, name="le%d" % s) for s in range(2)]
+        codes = [keep.tile([P, 4096], U32, name="codes%d" % s, align_bytes=64) for s in range(2)]
+        planes = [keep.tile([P, 4096], U8, name="planes%d" % s, align_bytes=64) for s in range(2)]
+        hp = (h1p, h2p)
+        ld = (l1d, l2d)
+
+        def generate(n, s):
+            he_w = he[s][:].bitcast(F32)
+            le_w = le[s][:].bitcast(F32)
+            nc.vector.tensor_copy(
+                out=he_w[:, 512 * n : 512 * n + 512].rearrange("p (k a w) -> p k a w", a=16, w=8),
+                in_=hp[s][:].bitcast(F32)[:, 32 * n : 32 * n + 32]
+                .rearrange("p (k w) -> p k w", w=8)
+                .unsqueeze(2)
+                .to_broadcast([P, 4, 16, 8]),
+            )
+            nc.scalar.copy(
+                out=le_w[:, 512 * n : 512 * n + 512].rearrange("p (k c) -> p k c", c=8),
+                in_=ld[s][:].bitcast(F32)[:, 64 * n : 64 * n + 64].unsqueeze(2).to_broadcast([P, 64, 8]),
+            )
+            hps = ps_h.tile([P, 512], F32, name="hps")
+            lps = ps_l.tile([P, 512], F32, name="lps")
+            for t in range(2):
+                for u in range(2):
+                    o = (2 * t + u) * P
+                    nc.tensor.transpose(hps[:, o : o + P], he_w[:, 512 * n + o : 512 * n + o + P], ident[:])
+            for g in range(2):
+                for t in range(2):
+                    o = (2 * g + t) * P
+                    i = 512 * n + 256 * t + P * g
+                    nc.tensor.transpose(lps[:, o : o + P], le_w[:, i : i + P], ident[:])
+            hs = work.tile([P, 1024], BF16, name="hs")
+            nc.scalar.copy(
+                out=hs[:].bitcast(F32).rearrange("p (t x u) -> p t x u", t=2, u=2),
+                in_=hps[:].rearrange("p (t u x) -> p t x u", t=2, u=2),
+            )
+            grouped = work.tile([P, 2048], BF16, name="grouped", align_bytes=64)
+            nc.vector.tensor_tensor(
+                out=grouped[:].rearrange("p (g w u e) -> p g w u e", g=2, u=2, e=2),
+                in0=lps[:]
+                .bitcast(BF16)
+                .rearrange("p (g w e) -> p g w e", g=2, e=2)
+                .unsqueeze(3)
+                .to_broadcast([P, 2, 256, 2, 2]),
+                in1=hs[:].rearrange("p (w u e) -> p w u e", u=2, e=2).unsqueeze(1).to_broadcast([P, 2, 256, 2, 2]),
+                op=MULT,
+            )
+            nc.vector.quantize_mx(
+                out=codes[s][:, 512 * n : 512 * n + 512].bitcast(FP8X4),
+                scales=planes[s][:, 512 * n : 512 * n + 512],
+                in_=grouped[:],
+            )
+
+        wg = keep.tile([P, 8192], BF16, name="wg", align_bytes=64)
+        wc = keep.tile([P, 2048], U32, name="wc", align_bytes=64)
+        ws = keep.tile([P, 2048], U8, name="ws", align_bytes=64)
+
+        def weights(g, g2):
+            nc.vector.tensor_copy(
+                out=wg[:, 4096 * g + 2048 * g2 : 4096 * g + 2048 * g2 + 2048].rearrange(
+                    "p (t b d j) -> p t b j d", t=4, b=16, d=8, j=4
+                ),
+                in_=wr[g][:, 2048 * g2 : 2048 * g2 + 2048].rearrange("p (b j t d) -> p t b j d", b=16, j=4, t=4, d=8),
+            )
+            o = 1024 * g + 512 * g2
+            nc.vector.quantize_mx(
+                out=wc[:, o : o + 512].bitcast(FP8X4),
+                scales=ws[:, o : o + 512],
+                in_=wg[:, 4 * o : 4 * o + 2048],
+            )
+
+        def score(n):
+            qg = work.tile([P, 2048], BF16, name="qg", align_bytes=64)
+            for g2 in range(2):
+                for t in range(2):
+                    acc = ps_1.tile([P, 512], F32, name="acc")
+                    for tt in range(4):
+                        for g in range(2):
+                            wo = 1024 * g + 512 * g2 + P * tt
+                            po = 512 * n + 256 * g + P * t
+                            nc.tensor.matmul_mx(
+                                out=acc[:, P * tt : P * tt + P],
+                                lhsT=wc[:, wo : wo + P].bitcast(FP8X4),
+                                lhsT_scale=ws[:, wo : wo + P],
+                                rhs=codes[0][:, po : po + P].bitcast(FP8X4),
+                                rhs_scale=planes[0][:, po : po + P],
+                                start=(g == 0),
+                                stop=(g == 1),
+                            )
+                    o = 1024 * g2 + 512 * t
+                    nc.scalar.copy(
+                        out=qg[:, o : o + 512].rearrange("p (w k) -> p w k", k=4),
+                        in_=acc[:].rearrange("p (k w) -> p w k", k=4),
+                    )
+            qc = work.tile([P, 512], U32, name="qc", align_bytes=64)
+            qs = work.tile([P, 512], U8, name="qs", align_bytes=64)
+            nc.vector.quantize_mx(out=qc[:].bitcast(FP8X4), scales=qs[:], in_=qg[:])
+            res = ps_2.tile([P, 512], F32, name="res")
+            for t in range(2):
+                for g2 in range(2):
+                    qo = 256 * g2 + P * t
+                    ro = 512 * n + 256 * g2
+                    nc.tensor.matmul_mx(
+                        out=res[:, 256 * t : 256 * t + 256],
+                        lhsT=qc[:, qo : qo + P].bitcast(FP8X4),
+                        lhsT_scale=qs[:, qo : qo + P],
+                        rhs=codes[1][:, ro : ro + 256].bitcast(FP8X4),
+                        rhs_scale=planes[1][:, ro : ro + 256],
+                        start=(g2 == 0),
+                        stop=(g2 == 1),
+                    )
+            ob = work.tile([P, 512], F32, name="ob")
+            nc.scalar.copy(
+                out=ob[:].rearrange("p (t x s) -> p t x s", t=2, s=2),
+                in_=res[:].rearrange("p (t s x) -> p t x s", t=2, s=2),
+            )
+            nc.sync.dma_start(out=out[n].rearrange("(x t) j -> x (t j)", t=2), in_=ob[:])
+
+        for n in range(NB + 1):
+            if n < NB:
+                generate(n, 0)
+                generate(n, 1)
+            if n == 0:
+                for g2 in range(2):
+                    for g in range(2):
+                        weights(g, g2)
+            if n >= 1:
+                score(n - 1)

@@ -15,6 +15,11 @@ MULT = mybir.AluOpType.mult
 
 P = 128
 NB = 8
+V = "vector"
+A = "scalar"
+PINNED = True
+LAG = 2
+WROUND = 1
 
 
 def tile_qriaffine_kernel(tc, layer1, layer2, layer3, h1, h2, h3, W, out):
@@ -26,6 +31,14 @@ def tile_qriaffine_kernel(tc, layer1, layer2, layer3, h1, h2, h3, W, out):
         ps_l = ctx.enter_context(tc.psum_pool(name="ps_l", bufs=2))
         ps_1 = ctx.enter_context(tc.psum_pool(name="ps_1", bufs=3))
         ps_2 = ctx.enter_context(tc.psum_pool(name="ps_2", bufs=1))
+        if PINNED:
+            ctx.enter_context(tc.manual_schedule())
+
+        def copy_on(engine, dst, src):
+            if engine == V:
+                nc.vector.tensor_copy(out=dst, in_=src)
+            else:
+                nc.scalar.copy(out=dst, in_=src)
 
         l1r = keep.tile([P, 16 * 32], BF16, name="l1r")
         h1r = keep.tile([P, 16 * 32], BF16, name="h1r")
@@ -51,25 +64,30 @@ def tile_qriaffine_kernel(tc, layer1, layer2, layer3, h1, h2, h3, W, out):
         l2d = keep.tile([P, 1024], BF16, name="l2d")
         h1p = keep.tile([P, 512], BF16, name="h1p")
         h2p = keep.tile([P, 512], BF16, name="h2p")
-        for ld, lr in ((l1d, l1r), (l2d, l2r)):
-            nc.vector.memset(ld[:], 1.0)
+        nc.vector.memset(l1d[:], 1.0)
+        nc.vector.memset(l2d[:], 1.0)
+
+        def prepare(s):
+            lsrc = (l1r, l2r)[s]
             nc.vector.tensor_copy(
-                out=ld[:].rearrange("p (n t a e) -> p n t a e", t=2, a=32, e=2)[:, :, :, 0:31, :],
-                in_=lr[:]
+                out=(l1d, l2d)[s][:].rearrange("p (n t a e) -> p n t a e", t=2, a=32, e=2)[:, :, :, 0:31, :],
+                in_=lsrc[:]
                 .rearrange("p (n f) -> p n f", n=NB)[:, :, 0:62]
                 .rearrange("p n (t a) -> p n t a", t=2)
                 .unsqueeze(4)
                 .to_broadcast([P, NB, 2, 31, 2]),
             )
-        for u in range(2):
-            nc.vector.tensor_copy(
-                out=h1p[:].rearrange("p (k u c e) -> p k u c e", u=2, c=8, e=2)[:, :, u, :, :],
-                in_=h1r[:].rearrange("p (k c u e) -> p k u c e", c=8, u=2, e=2)[:, :, u, :, :],
-            )
-            nc.vector.tensor_copy(
-                out=h2p[:].rearrange("p (k u d e) -> p k u d e", u=2, d=8, e=2)[:, :, u, :, :],
-                in_=h2r[:].rearrange("p (k u e d) -> p k u d e", u=2, e=2, d=8)[:, :, u, :, :],
-            )
+            for u in range(2):
+                if s == 0:
+                    nc.vector.tensor_copy(
+                        out=h1p[:].rearrange("p (k u c e) -> p k u c e", u=2, c=8, e=2)[:, :, u, :, :],
+                        in_=h1r[:].rearrange("p (k c u e) -> p k u c e", c=8, u=2, e=2)[:, :, u, :, :],
+                    )
+                else:
+                    nc.vector.tensor_copy(
+                        out=h2p[:].rearrange("p (k u d e) -> p k u d e", u=2, d=8, e=2)[:, :, u, :, :],
+                        in_=h2r[:].rearrange("p (k u e d) -> p k u d e", u=2, e=2, d=8)[:, :, u, :, :],
+                    )
 
         he = [keep.tile([P, 8192], BF16, name="he%d" % s) for s in range(2)]
         le = [keep.tile([P, 8192], BF16, name="le%d" % s) for s in range(2)]
@@ -77,21 +95,29 @@ def tile_qriaffine_kernel(tc, layer1, layer2, layer3, h1, h2, h3, W, out):
         planes = [keep.tile([P, 4096], U8, name="planes%d" % s, align_bytes=64) for s in range(2)]
         hp = (h1p, h2p)
         ld = (l1d, l2d)
+        live = {}
 
-        def generate(n, s):
-            he_w = he[s][:].bitcast(F32)
-            le_w = le[s][:].bitcast(F32)
-            nc.vector.tensor_copy(
-                out=he_w[:, 512 * n : 512 * n + 512].rearrange("p (k a w) -> p k a w", a=16, w=8),
-                in_=hp[s][:].bitcast(F32)[:, 32 * n : 32 * n + 32]
+        def spread_h(n, s, engine):
+            copy_on(
+                engine,
+                he[s][:].bitcast(F32)[:, 512 * n : 512 * n + 512].rearrange("p (k a w) -> p k a w", a=16, w=8),
+                hp[s][:]
+                .bitcast(F32)[:, 32 * n : 32 * n + 32]
                 .rearrange("p (k w) -> p k w", w=8)
                 .unsqueeze(2)
                 .to_broadcast([P, 4, 16, 8]),
             )
-            nc.scalar.copy(
-                out=le_w[:, 512 * n : 512 * n + 512].rearrange("p (k c) -> p k c", c=8),
-                in_=ld[s][:].bitcast(F32)[:, 64 * n : 64 * n + 64].unsqueeze(2).to_broadcast([P, 64, 8]),
+
+        def spread_l(n, s, engine):
+            copy_on(
+                engine,
+                le[s][:].bitcast(F32)[:, 512 * n : 512 * n + 512].rearrange("p (k c) -> p k c", c=8),
+                ld[s][:].bitcast(F32)[:, 64 * n : 64 * n + 64].unsqueeze(2).to_broadcast([P, 64, 8]),
             )
+
+        def flip(n, s):
+            he_w = he[s][:].bitcast(F32)
+            le_w = le[s][:].bitcast(F32)
             hps = ps_h.tile([P, 512], F32, name="hps")
             lps = ps_l.tile([P, 512], F32, name="lps")
             for t in range(2):
@@ -103,39 +129,58 @@ def tile_qriaffine_kernel(tc, layer1, layer2, layer3, h1, h2, h3, W, out):
                     o = (2 * g + t) * P
                     i = 512 * n + 256 * t + P * g
                     nc.tensor.transpose(lps[:, o : o + P], le_w[:, i : i + P], ident[:])
+            live["hps", n, s] = hps
+            live["lps", n, s] = lps
+
+        def fetch_h(n, s, engine):
             hs = work.tile([P, 1024], BF16, name="hs")
-            nc.scalar.copy(
-                out=hs[:].bitcast(F32).rearrange("p (t x u) -> p t x u", t=2, u=2),
-                in_=hps[:].rearrange("p (t u x) -> p t x u", t=2, u=2),
+            copy_on(
+                engine,
+                hs[:].bitcast(F32).rearrange("p (t x u) -> p t x u", t=2, u=2),
+                live["hps", n, s][:].rearrange("p (t u x) -> p t x u", t=2, u=2),
             )
+            live["hs", n, s] = hs
+
+        def multiply(n, s):
             grouped = work.tile([P, 2048], BF16, name="grouped", align_bytes=64)
             nc.vector.tensor_tensor(
                 out=grouped[:].rearrange("p (g w u e) -> p g w u e", g=2, u=2, e=2),
-                in0=lps[:]
+                in0=live["lps", n, s][:]
                 .bitcast(BF16)
                 .rearrange("p (g w e) -> p g w e", g=2, e=2)
                 .unsqueeze(3)
                 .to_broadcast([P, 2, 256, 2, 2]),
-                in1=hs[:].rearrange("p (w u e) -> p w u e", u=2, e=2).unsqueeze(1).to_broadcast([P, 2, 256, 2, 2]),
+                in1=live["hs", n, s][:]
+                .rearrange("p (w u e) -> p w u e", u=2, e=2)
+                .unsqueeze(1)
+                .to_broadcast([P, 2, 256, 2, 2]),
                 op=MULT,
             )
+            live["grouped", n, s] = grouped
+
+        def quantise(n, s):
             nc.vector.quantize_mx(
                 out=codes[s][:, 512 * n : 512 * n + 512].bitcast(FP8X4),
                 scales=planes[s][:, 512 * n : 512 * n + 512],
-                in_=grouped[:],
+                in_=live["grouped", n, s][:],
             )
 
         wg = keep.tile([P, 8192], BF16, name="wg", align_bytes=64)
         wc = keep.tile([P, 2048], U32, name="wc", align_bytes=64)
         ws = keep.tile([P, 2048], U8, name="ws", align_bytes=64)
 
-        def weights(g, g2):
-            nc.vector.tensor_copy(
-                out=wg[:, 4096 * g + 2048 * g2 : 4096 * g + 2048 * g2 + 2048].rearrange(
-                    "p (t b d j) -> p t b j d", t=4, b=16, d=8, j=4
-                ),
-                in_=wr[g][:, 2048 * g2 : 2048 * g2 + 2048].rearrange("p (b j t d) -> p t b j d", b=16, j=4, t=4, d=8),
+        def regroup_w(g, g2, engine):
+            dst = wg[:, 4096 * g + 2048 * g2 : 4096 * g + 2048 * g2 + 2048].rearrange(
+                "p (t b d j) -> p t b j d", t=4, b=16, d=8, j=4
             )
+            src = wr[g][:, 2048 * g2 : 2048 * g2 + 2048].rearrange("p (b j t d) -> p t b j d", b=16, j=4, t=4, d=8)
+            if engine == V:
+                nc.vector.tensor_copy(out=dst, in_=src)
+            else:
+                for t in range(4):
+                    nc.scalar.copy(out=dst[:, t], in_=src[:, t])
+
+        def quantise_w(g, g2):
             o = 1024 * g + 512 * g2
             nc.vector.quantize_mx(
                 out=wc[:, o : o + 512].bitcast(FP8X4),
@@ -143,32 +188,42 @@ def tile_qriaffine_kernel(tc, layer1, layer2, layer3, h1, h2, h3, W, out):
                 in_=wg[:, 4 * o : 4 * o + 2048],
             )
 
-        def score(n):
-            qg = work.tile([P, 2048], BF16, name="qg", align_bytes=64)
-            for g2 in range(2):
-                for t in range(2):
-                    acc = ps_1.tile([P, 512], F32, name="acc")
-                    for tt in range(4):
-                        for g in range(2):
-                            wo = 1024 * g + 512 * g2 + P * tt
-                            po = 512 * n + 256 * g + P * t
-                            nc.tensor.matmul_mx(
-                                out=acc[:, P * tt : P * tt + P],
-                                lhsT=wc[:, wo : wo + P].bitcast(FP8X4),
-                                lhsT_scale=ws[:, wo : wo + P],
-                                rhs=codes[0][:, po : po + P].bitcast(FP8X4),
-                                rhs_scale=planes[0][:, po : po + P],
-                                start=(g == 0),
-                                stop=(g == 1),
-                            )
-                    o = 1024 * g2 + 512 * t
-                    nc.scalar.copy(
-                        out=qg[:, o : o + 512].rearrange("p (w k) -> p w k", k=4),
-                        in_=acc[:].rearrange("p (k w) -> p w k", k=4),
+        def first_product(n, b):
+            g2, t = divmod(b, 2)
+            acc = ps_1.tile([P, 512], F32, name="acc")
+            for tt in range(4):
+                for g in range(2):
+                    wo = 1024 * g + 512 * g2 + P * tt
+                    po = 512 * n + 256 * g + P * t
+                    nc.tensor.matmul_mx(
+                        out=acc[:, P * tt : P * tt + P],
+                        lhsT=wc[:, wo : wo + P].bitcast(FP8X4),
+                        lhsT_scale=ws[:, wo : wo + P],
+                        rhs=codes[0][:, po : po + P].bitcast(FP8X4),
+                        rhs_scale=planes[0][:, po : po + P],
+                        start=(g == 0),
+                        stop=(g == 1),
                     )
+            live["acc", n, b] = acc
+
+        def fetch_q(n, b, engine):
+            if b == 0:
+                qg = work.tile([P, 2048], BF16, name="qg", align_bytes=64)
+                live["qg", n] = qg
+            copy_on(
+                engine,
+                live["qg", n][:, 512 * b : 512 * b + 512].rearrange("p (w k) -> p w k", k=4),
+                live["acc", n, b][:].rearrange("p (k w) -> p w k", k=4),
+            )
+
+        def quantise_q(n):
             qc = work.tile([P, 512], U32, name="qc", align_bytes=64)
             qs = work.tile([P, 512], U8, name="qs", align_bytes=64)
-            nc.vector.quantize_mx(out=qc[:].bitcast(FP8X4), scales=qs[:], in_=qg[:])
+            nc.vector.quantize_mx(out=qc[:].bitcast(FP8X4), scales=qs[:], in_=live["qg", n][:])
+            live["qc", n] = qc
+            live["qs", n] = qs
+
+        def second_product(n):
             res = ps_2.tile([P, 512], F32, name="res")
             for t in range(2):
                 for g2 in range(2):
@@ -176,27 +231,59 @@ def tile_qriaffine_kernel(tc, layer1, layer2, layer3, h1, h2, h3, W, out):
                     ro = 512 * n + 256 * g2
                     nc.tensor.matmul_mx(
                         out=res[:, 256 * t : 256 * t + 256],
-                        lhsT=qc[:, qo : qo + P].bitcast(FP8X4),
-                        lhsT_scale=qs[:, qo : qo + P],
+                        lhsT=live["qc", n][:, qo : qo + P].bitcast(FP8X4),
+                        lhsT_scale=live["qs", n][:, qo : qo + P],
                         rhs=codes[1][:, ro : ro + 256].bitcast(FP8X4),
                         rhs_scale=planes[1][:, ro : ro + 256],
                         start=(g2 == 0),
                         stop=(g2 == 1),
                     )
+            live["res", n] = res
+
+        def deliver(n, engine):
             ob = work.tile([P, 512], F32, name="ob")
-            nc.scalar.copy(
-                out=ob[:].rearrange("p (t x s) -> p t x s", t=2, s=2),
-                in_=res[:].rearrange("p (t s x) -> p t x s", t=2, s=2),
+            copy_on(
+                engine,
+                ob[:].rearrange("p (t x s) -> p t x s", t=2, s=2),
+                live["res", n][:].rearrange("p (t s x) -> p t x s", t=2, s=2),
             )
             nc.sync.dma_start(out=out[n].rearrange("(x t) j -> x (t j)", t=2), in_=ob[:])
 
-        for n in range(NB + 1):
-            if n < NB:
-                generate(n, 0)
-                generate(n, 1)
-            if n == 0:
-                for g2 in range(2):
-                    for g in range(2):
-                        weights(g, g2)
-            if n >= 1:
-                score(n - 1)
+        prepare(0)
+        prepare(1)
+        for s in range(2):
+            spread_l(0, s, A)
+            spread_h(0, s, V)
+        for r in range(NB + LAG + 1):
+            n = r - LAG
+            if 0 <= n - 1:
+                quantise_q(n - 1)
+            if r + 1 < NB:
+                spread_l(r + 1, 0, A)
+                spread_h(r + 1, 0, V)
+                spread_h(r + 1, 1, V)
+            if r < NB:
+                flip(r, 0)
+                fetch_h(r, 0, A)
+                flip(r, 1)
+                fetch_h(r, 1, A)
+            if r + 1 < NB:
+                spread_l(r + 1, 1, A)
+            if r < NB:
+                multiply(r, 0)
+                multiply(r, 1)
+                quantise(r, 0)
+                quantise(r, 1)
+            if r == WROUND:
+                for g in range(2):
+                    regroup_w(g, 0, V)
+                    regroup_w(g, 1, A)
+                    quantise_w(g, 0)
+                    quantise_w(g, 1)
+            if 0 <= n < NB:
+                for b in range(4):
+                    first_product(n, b)
+                    fetch_q(n, b, A)
+            if 0 <= n - 1:
+                second_product(n - 1)
+                deliver(n - 1, A)

@@ -18,8 +18,9 @@ NB = 8
 V = "vector"
 A = "scalar"
 PINNED = True
-LAG = 2
-WROUND = 1
+NCHIP = 2
+NHE = 1
+WSPLIT = 1
 
 
 def tile_qriaffine_kernel(tc, layer1, layer2, layer3, h1, h2, h3, W, out):
@@ -28,8 +29,7 @@ def tile_qriaffine_kernel(tc, layer1, layer2, layer3, h1, h2, h3, W, out):
         keep = ctx.enter_context(tc.tile_pool(name="keep", bufs=1))
         work = ctx.enter_context(tc.tile_pool(name="work", bufs=3))
         ps_h = ctx.enter_context(tc.psum_pool(name="ps_h", bufs=2))
-        ps_l = ctx.enter_context(tc.psum_pool(name="ps_l", bufs=2))
-        ps_1 = ctx.enter_context(tc.psum_pool(name="ps_1", bufs=3))
+        ps_1 = ctx.enter_context(tc.psum_pool(name="ps_1", bufs=5))
         ps_2 = ctx.enter_context(tc.psum_pool(name="ps_2", bufs=1))
         if PINNED:
             ctx.enter_context(tc.manual_schedule())
@@ -40,73 +40,100 @@ def tile_qriaffine_kernel(tc, layer1, layer2, layer3, h1, h2, h3, W, out):
             else:
                 nc.scalar.copy(out=dst, in_=src)
 
-        l1r = keep.tile([P, 16 * 32], BF16, name="l1r")
-        h1r = keep.tile([P, 16 * 32], BF16, name="h1r")
-        l2r = keep.tile([P, 16 * 32], BF16, name="l2r")
-        h2r = keep.tile([P, 16 * 32], BF16, name="h2r")
-        for dst, src, width in ((l1r, layer1, 62), (h1r, h1, 64), (l2r, layer2, 62), (h2r, h2, 64)):
-            nc.scalar.dma_start(
-                out=dst[:].rearrange("p (n f) -> p n f", n=NB)[:, :, 0:width],
-                in_=src.rearrange("n (x t) a -> x n (t a)", t=2),
-            )
+        lr = [keep.tile([P, 512], BF16, name="lr%d" % s) for s in range(2)]
+        hr = [keep.tile([P, 512], BF16, name="hr%d" % s) for s in range(2)]
         wr = [keep.tile([P, 4096], BF16, name="wr%d" % g) for g in range(2)]
-        for g in range(2):
-            for c8 in range(8):
-                nc.sync.dma_start(
-                    out=wr[g][c8:P:8, :].rearrange("p (b f) -> p b f", b=32),
-                    in_=W[16 * g : 16 * g + 16, :, 4 * c8 : 4 * c8 + 4, :].rearrange("a b j d -> a b (j d)"),
+        ident = keep.tile([P, P], F32, name="ident")
+        identb = keep.tile([P, P], BF16, name="identb")
+        selh = keep.tile([P, 2048], BF16, name="selh")
+        ld = [keep.tile([P, 1024], BF16, name="ld%d" % s) for s in range(2)]
+        hq = [keep.tile([P, 512], BF16, name="hq%d" % s) for s in range(2)]
+        zs = [keep.tile([P, 256], F32, name="zs%d" % s) for s in range(2)]
+        ys = [keep.tile([P, 512], F32, name="ys%d" % s) for s in range(2)]
+        hx = [keep.tile([P, NHE * 1024], BF16, name="hx%d" % s) for s in range(2)]
+        le = [keep.tile([P, NCHIP * 1024], BF16, name="le%d" % s) for s in range(2)]
+        ldd = [keep.tile([P, (NB - NCHIP) * 1024], BF16, name="ldd%d" % s) for s in range(2)]
+        codes = [keep.tile([P, 4096], U32, name="codes%d" % s, align_bytes=64) for s in range(2)]
+        planes = [keep.tile([P, 4096], U8, name="planes%d" % s, align_bytes=64) for s in range(2)]
+        wg = keep.tile([P, 8192], BF16, name="wg", align_bytes=64)
+        wc = keep.tile([P, 2048], U32, name="wc", align_bytes=64)
+        ws = keep.tile([P, 2048], U8, name="ws", align_bytes=64)
+        live = {}
+
+        def load_x(s):
+            nc.scalar.dma_start(
+                out=hr[s][:].rearrange("p (n f) -> p n f", n=NB),
+                in_=(h1, h2)[s].rearrange("n (x t) a -> x n (t a)", t=2),
+            )
+            nc.scalar.dma_start(
+                out=lr[s][:].rearrange("p (n f) -> p n f", n=NB)[:, :, 0:62],
+                in_=(layer1, layer2)[s].rearrange("n (x t) a -> x n (t a)", t=2),
+            )
+
+        def load_w(g, c8):
+            nc.sync.dma_start(
+                out=wr[g][c8:P:8, :].rearrange("p (b f) -> p b f", b=32),
+                in_=W[16 * g : 16 * g + 16, :, 4 * c8 : 4 * c8 + 4, :].rearrange("a b j d -> a b (j d)"),
+            )
+
+        def constants():
+            make_identity(nc, ident[:])
+            make_identity(nc, identb[:])
+            nc.gpsimd.memset(ld[0][:], 1.0)
+            nc.gpsimd.memset(ld[1][:], 1.0)
+            nc.vector.tensor_copy(
+                out=selh[:].rearrange("p (k a c) -> p k a c", k=16, a=16, c=8),
+                in_=identb[:].rearrange("p (c k) -> p k c", c=8, k=16).unsqueeze(2).to_broadcast([P, 16, 16, 8]),
+            )
+
+        def permute_h(s):
+            for u in range(2):
+                if s == 0:
+                    src = hr[0][:].rearrange("p (k c u e) -> p u c k e", c=8, u=2, e=2)[:, u]
+                else:
+                    src = hr[1][:].rearrange("p (k u e d) -> p u d k e", u=2, e=2, d=8)[:, u]
+                nc.vector.tensor_copy(
+                    out=hq[s][:].rearrange("p (u c k e) -> p u c k e", u=2, c=8, k=16, e=2)[:, u], in_=src
                 )
 
-        ident = keep.tile([P, P], F32, name="ident")
-        make_identity(nc, ident[:])
+        def flip_h(s, engine):
+            zps = ps_1.tile([P, 512], F32, name="acc")
+            for u in range(2):
+                nc.tensor.transpose(zps[:, P * u : P * u + P], hq[s][:].bitcast(F32)[:, P * u : P * u + P], ident[:])
+            copy_on(
+                engine,
+                zs[s][:].rearrange("p (x u) -> p x u", u=2),
+                zps[:, 0:256].rearrange("p (u x) -> p x u", u=2),
+            )
 
-        l1d = keep.tile([P, 1024], BF16, name="l1d")
-        l2d = keep.tile([P, 1024], BF16, name="l2d")
-        h1p = keep.tile([P, 512], BF16, name="h1p")
-        h2p = keep.tile([P, 512], BF16, name="h2p")
-        nc.vector.memset(l1d[:], 1.0)
-        nc.vector.memset(l2d[:], 1.0)
-
-        def prepare(s):
-            lsrc = (l1r, l2r)[s]
+        def prepare_l(s):
             nc.vector.tensor_copy(
-                out=(l1d, l2d)[s][:].rearrange("p (n t a e) -> p n t a e", t=2, a=32, e=2)[:, :, :, 0:31, :],
-                in_=lsrc[:]
+                out=ld[s][:].rearrange("p (n t a e) -> p n t a e", t=2, a=32, e=2)[:, :, :, 0:31, :],
+                in_=lr[s][:]
                 .rearrange("p (n f) -> p n f", n=NB)[:, :, 0:62]
                 .rearrange("p n (t a) -> p n t a", t=2)
                 .unsqueeze(4)
                 .to_broadcast([P, NB, 2, 31, 2]),
             )
-            for u in range(2):
-                if s == 0:
-                    nc.vector.tensor_copy(
-                        out=h1p[:].rearrange("p (k u c e) -> p k u c e", u=2, c=8, e=2)[:, :, u, :, :],
-                        in_=h1r[:].rearrange("p (k c u e) -> p k u c e", c=8, u=2, e=2)[:, :, u, :, :],
-                    )
-                else:
-                    nc.vector.tensor_copy(
-                        out=h2p[:].rearrange("p (k u d e) -> p k u d e", u=2, d=8, e=2)[:, :, u, :, :],
-                        in_=h2r[:].rearrange("p (k u e d) -> p k u d e", u=2, e=2, d=8)[:, :, u, :, :],
-                    )
 
-        he = [keep.tile([P, 8192], BF16, name="he%d" % s) for s in range(2)]
-        le = [keep.tile([P, 8192], BF16, name="le%d" % s) for s in range(2)]
-        codes = [keep.tile([P, 4096], U32, name="codes%d" % s, align_bytes=64) for s in range(2)]
-        planes = [keep.tile([P, 4096], U8, name="planes%d" % s, align_bytes=64) for s in range(2)]
-        hp = (h1p, h2p)
-        ld = (l1d, l2d)
-        live = {}
-
-        def spread_h(n, s, engine):
-            copy_on(
-                engine,
-                he[s][:].bitcast(F32)[:, 512 * n : 512 * n + 512].rearrange("p (k a w) -> p k a w", a=16, w=8),
-                hp[s][:]
-                .bitcast(F32)[:, 32 * n : 32 * n + 32]
-                .rearrange("p (k w) -> p k w", w=8)
-                .unsqueeze(2)
-                .to_broadcast([P, 4, 16, 8]),
+        def park_l(s, engine):
+            yps = ps_1.tile([P, 512], F32, name="acc")
+            for j in range(4):
+                nc.tensor.transpose(yps[:, P * j : P * j + P], ld[s][:].bitcast(F32)[:, P * j : P * j + P], ident[:])
+            copy_on(engine, ys[s][:], yps[:])
+            nc.gpsimd.dma_start(
+                out=out[NB - 2 + s].rearrange("(j h) (q x) -> (h q) j x", j=4, q=2),
+                in_=ys[s][:].rearrange("p (j x) -> p j x", j=4),
             )
+
+        def fetch_l(s, n0, n1):
+            for c8 in range(8):
+                nc.sync.dma_start(
+                    out=ldd[s][:]
+                    .bitcast(F32)[c8:P:8, 512 * (n0 - NCHIP) : 512 * (n1 - NCHIP)]
+                    .rearrange("p (r x) -> p r x", x=P),
+                    in_=out[NB - 2 + s].rearrange("(r h) (q x) -> (h q) r x", h=8, q=2)[:, 4 * n0 : 4 * n1, :],
+                )
 
         def spread_l(n, s, engine):
             copy_on(
@@ -115,45 +142,70 @@ def tile_qriaffine_kernel(tc, layer1, layer2, layer3, h1, h2, h3, W, out):
                 ld[s][:].bitcast(F32)[:, 64 * n : 64 * n + 64].unsqueeze(2).to_broadcast([P, 64, 8]),
             )
 
-        def flip(n, s):
-            he_w = he[s][:].bitcast(F32)
-            le_w = le[s][:].bitcast(F32)
-            hps = ps_h.tile([P, 512], F32, name="hps")
-            lps = ps_l.tile([P, 512], F32, name="lps")
-            for t in range(2):
-                for u in range(2):
-                    o = (2 * t + u) * P
-                    nc.tensor.transpose(hps[:, o : o + P], he_w[:, 512 * n + o : 512 * n + o + P], ident[:])
-            for g in range(2):
-                for t in range(2):
-                    o = (2 * g + t) * P
-                    i = 512 * n + 256 * t + P * g
-                    nc.tensor.transpose(lps[:, o : o + P], le_w[:, i : i + P], ident[:])
-            live["hps", n, s] = hps
-            live["lps", n, s] = lps
+        def flip_l(n, s, engine):
+            lps = ps_1.tile([P, 512], F32, name="acc")
+            for o in range(0, 512, P):
+                nc.tensor.transpose(lps[:, o : o + P], le[s][:].bitcast(F32)[:, 512 * n + o : 512 * n + o + P], ident[:])
+            ls = work.tile([P, 1024], BF16, name="ls", bufs=2 * NCHIP)
+            copy_on(engine, ls[:].bitcast(F32), lps[:])
+            live["ls", n, s] = ls
 
-        def fetch_h(n, s, engine):
-            hs = work.tile([P, 1024], BF16, name="hs")
-            copy_on(
-                engine,
-                hs[:].bitcast(F32).rearrange("p (t x u) -> p t x u", t=2, u=2),
-                live["hps", n, s][:].rearrange("p (t u x) -> p t x u", t=2, u=2),
+        def spread_h(n, s):
+            nc.vector.tensor_copy(
+                out=hx[s][:].bitcast(F32)[:, 512 * n : 512 * n + 512].rearrange("p (t u a c) -> p t u a c", t=2, u=2, a=16),
+                in_=hq[s][:]
+                .bitcast(F32)
+                .rearrange("p (u c k) -> p k u c", u=2, c=8)[:, 2 * n : 2 * n + 2]
+                .unsqueeze(3)
+                .to_broadcast([P, 2, 2, 16, 8]),
             )
-            live["hs", n, s] = hs
+
+        def select_h(n, s):
+            if n < NHE:
+                hpf = ps_h.tile([P, 512], F32, name="hps")
+                for o in range(0, 512, P):
+                    nc.tensor.transpose(
+                        hpf[:, o : o + P], hx[s][:].bitcast(F32)[:, 512 * n + o : 512 * n + o + P], ident[:]
+                    )
+                live["hps", n, s] = hpf
+                return
+            hps = ps_h.tile([P, 1024], BF16, name="hps")
+            for t in range(2):
+                k = 2 * n + t
+                nc.tensor.matmul(
+                    out=hps[:, 512 * t : 512 * t + 512],
+                    lhsT=selh[:, P * k : P * k + P],
+                    rhs=zs[s][:].bitcast(BF16),
+                    start=True,
+                    stop=True,
+                )
+            live["hps", n, s] = hps
 
         def multiply(n, s):
             grouped = work.tile([P, 2048], BF16, name="grouped", align_bytes=64)
+            lsrc = live["ls", n, s][:] if n < NCHIP else ldd[s][:, 1024 * (n - NCHIP) : 1024 * (n - NCHIP) + 1024]
+            live["grouped", n, s] = grouped
+            if n < NHE:
+                for t in range(2):
+                    for g in range(2):
+                        nc.vector.tensor_tensor(
+                            out=grouped[:].rearrange("p (t g x u e) -> p t g x u e", t=2, g=2, u=2, e=2)[:, t, g],
+                            in0=live["hps", n, s][:]
+                            .bitcast(BF16)
+                            .rearrange("p (t u x e) -> p t x u e", t=2, u=2, e=2)[:, t],
+                            in1=lsrc.rearrange("p (t g x e) -> p t g x e", t=2, g=2, e=2)[:, t, g]
+                            .unsqueeze(2)
+                            .to_broadcast([P, P, 2, 2]),
+                            op=MULT,
+                        )
+                return
             nc.vector.tensor_tensor(
-                out=grouped[:].rearrange("p (g w u e) -> p g w u e", g=2, u=2, e=2),
-                in0=live["lps", n, s][:]
-                .bitcast(BF16)
-                .rearrange("p (g w e) -> p g w e", g=2, e=2)
-                .unsqueeze(3)
-                .to_broadcast([P, 2, 256, 2, 2]),
-                in1=live["hs", n, s][:]
-                .rearrange("p (w u e) -> p w u e", u=2, e=2)
-                .unsqueeze(1)
-                .to_broadcast([P, 2, 256, 2, 2]),
+                out=grouped[:].rearrange("p (t g x u e) -> p t g x u e", t=2, g=2, u=2, e=2),
+                in0=live["hps", n, s][:]
+                .rearrange("p (t x u e) -> p t x u e", t=2, u=2, e=2)
+                .unsqueeze(2)
+                .to_broadcast([P, 2, 2, P, 2, 2]),
+                in1=lsrc.rearrange("p (t g x e) -> p t g x e", t=2, g=2, e=2).unsqueeze(4).to_broadcast([P, 2, 2, P, 2, 2]),
                 op=MULT,
             )
             live["grouped", n, s] = grouped
@@ -165,19 +217,15 @@ def tile_qriaffine_kernel(tc, layer1, layer2, layer3, h1, h2, h3, W, out):
                 in_=live["grouped", n, s][:],
             )
 
-        wg = keep.tile([P, 8192], BF16, name="wg", align_bytes=64)
-        wc = keep.tile([P, 2048], U32, name="wc", align_bytes=64)
-        ws = keep.tile([P, 2048], U8, name="ws", align_bytes=64)
-
-        def regroup_w(g, g2, engine):
+        def regroup_w(g, g2, engine, t0=0, t1=4):
             dst = wg[:, 4096 * g + 2048 * g2 : 4096 * g + 2048 * g2 + 2048].rearrange(
                 "p (t b d j) -> p t b j d", t=4, b=16, d=8, j=4
             )
             src = wr[g][:, 2048 * g2 : 2048 * g2 + 2048].rearrange("p (b j t d) -> p t b j d", b=16, j=4, t=4, d=8)
             if engine == V:
-                nc.vector.tensor_copy(out=dst, in_=src)
+                nc.vector.tensor_copy(out=dst[:, t0:t1], in_=src[:, t0:t1])
             else:
-                for t in range(4):
+                for t in range(t0, t1):
                     nc.scalar.copy(out=dst[:, t], in_=src[:, t])
 
         def quantise_w(g, g2):
@@ -194,7 +242,7 @@ def tile_qriaffine_kernel(tc, layer1, layer2, layer3, h1, h2, h3, W, out):
             for tt in range(4):
                 for g in range(2):
                     wo = 1024 * g + 512 * g2 + P * tt
-                    po = 512 * n + 256 * g + P * t
+                    po = 512 * n + 256 * t + P * g
                     nc.tensor.matmul_mx(
                         out=acc[:, P * tt : P * tt + P],
                         lhsT=wc[:, wo : wo + P].bitcast(FP8X4),
@@ -207,7 +255,7 @@ def tile_qriaffine_kernel(tc, layer1, layer2, layer3, h1, h2, h3, W, out):
             live["acc", n, b] = acc
 
         def fetch_q(n, b, engine):
-            if b == 0:
+            if ("qg", n) not in live:
                 qg = work.tile([P, 2048], BF16, name="qg", align_bytes=64)
                 live["qg", n] = qg
             copy_on(
@@ -225,19 +273,20 @@ def tile_qriaffine_kernel(tc, layer1, layer2, layer3, h1, h2, h3, W, out):
 
         def second_product(n):
             res = ps_2.tile([P, 512], F32, name="res")
-            for t in range(2):
-                for g2 in range(2):
-                    qo = 256 * g2 + P * t
-                    ro = 512 * n + 256 * g2
-                    nc.tensor.matmul_mx(
-                        out=res[:, 256 * t : 256 * t + 256],
-                        lhsT=live["qc", n][:, qo : qo + P].bitcast(FP8X4),
-                        lhsT_scale=live["qs", n][:, qo : qo + P],
-                        rhs=codes[1][:, ro : ro + 256].bitcast(FP8X4),
-                        rhs_scale=planes[1][:, ro : ro + 256],
-                        start=(g2 == 0),
-                        stop=(g2 == 1),
-                    )
+            for ti in range(2):
+                for tj in range(2):
+                    for g2 in range(2):
+                        qo = 256 * g2 + P * ti
+                        ro = 512 * n + 256 * tj + P * g2
+                        nc.tensor.matmul_mx(
+                            out=res[:, 256 * ti + P * tj : 256 * ti + P * tj + P],
+                            lhsT=live["qc", n][:, qo : qo + P].bitcast(FP8X4),
+                            lhsT_scale=live["qs", n][:, qo : qo + P],
+                            rhs=codes[1][:, ro : ro + P].bitcast(FP8X4),
+                            rhs_scale=planes[1][:, ro : ro + P],
+                            start=(g2 == 0),
+                            stop=(g2 == 1),
+                        )
             live["res", n] = res
 
         def deliver(n, engine):
@@ -249,41 +298,67 @@ def tile_qriaffine_kernel(tc, layer1, layer2, layer3, h1, h2, h3, W, out):
             )
             nc.sync.dma_start(out=out[n].rearrange("(x t) j -> x (t j)", t=2), in_=ob[:])
 
-        prepare(0)
-        prepare(1)
+        load_x(0)
+        load_x(1)
+        for g in range(2):
+            for c8 in range(8):
+                load_w(g, c8)
+        constants()
         for s in range(2):
-            spread_l(0, s, A)
-            spread_h(0, s, V)
-        for r in range(NB + LAG + 1):
-            n = r - LAG
+            permute_h(s)
+            spread_h(0, s)
+            select_h(0, s)
+            prepare_l(s)
+            spread_l(0, s, V)
+            flip_l(0, s, A)
+            flip_h(s, A)
+            park_l(s, A)
+        for s in range(2):
+            fetch_l(s, NCHIP, 4)
+        for s in range(2):
+            fetch_l(s, 4, NB)
+        multiply(0, 0)
+        multiply(0, 1)
+        for n in range(1, NCHIP):
+            for s in range(2):
+                spread_l(n, s, A)
+                flip_l(n, s, A)
+        quantise(0, 0)
+        quantise(0, 1)
+        select_h(1, 0)
+        select_h(1, 1)
+        regroup_w(0, 0, V)
+        regroup_w(0, 1, A)
+        multiply(1, 0)
+        select_h(2, 0)
+        quantise_w(0, 0)
+        quantise_w(0, 1)
+        regroup_w(1, 0, V)
+        regroup_w(1, 1, V, 0, WSPLIT)
+        regroup_w(1, 1, A, WSPLIT, 4)
+        quantise_w(1, 0)
+        quantise_w(1, 1)
+        quantise(1, 0)
+        multiply(1, 1)
+        quantise(1, 1)
+        for r in range(1, NB + 2):
+            n = r - 1
+            if 2 <= r < NB:
+                multiply(r, 0)
             if 0 <= n - 1:
                 quantise_q(n - 1)
-            if r + 1 < NB:
-                spread_l(r + 1, 0, A)
-                spread_h(r + 1, 0, V)
-                spread_h(r + 1, 1, V)
-            if r < NB:
-                flip(r, 0)
-                fetch_h(r, 0, A)
-                flip(r, 1)
-                fetch_h(r, 1, A)
-            if r + 1 < NB:
-                spread_l(r + 1, 1, A)
-            if r < NB:
-                multiply(r, 0)
+            if 2 <= r < NB:
                 multiply(r, 1)
                 quantise(r, 0)
                 quantise(r, 1)
-            if r == WROUND:
-                for g in range(2):
-                    regroup_w(g, 0, V)
-                    regroup_w(g, 1, A)
-                    quantise_w(g, 0)
-                    quantise_w(g, 1)
-            if 0 <= n < NB:
+            if n < NB:
                 for b in range(4):
                     first_product(n, b)
                     fetch_q(n, b, A)
             if 0 <= n - 1:
                 second_product(n - 1)
                 deliver(n - 1, A)
+            if r + 1 < NB:
+                if r > 1:
+                    select_h(r + 1, 0)
+                select_h(r + 1, 1)

@@ -20,7 +20,7 @@ A = "scalar"
 PINNED = True
 NCHIP = 2
 NHE = 1
-WSPLIT = 1
+WSPLIT = 2
 
 
 def tile_qriaffine_kernel(tc, layer1, layer2, layer3, h1, h2, h3, W, out):
@@ -49,6 +49,7 @@ def tile_qriaffine_kernel(tc, layer1, layer2, layer3, h1, h2, h3, W, out):
         ld = [keep.tile([P, 1024], BF16, name="ld%d" % s) for s in range(2)]
         hq = [keep.tile([P, 512], BF16, name="hq%d" % s) for s in range(2)]
         zs = [keep.tile([P, 256], F32, name="zs%d" % s) for s in range(2)]
+        lq = [keep.tile([P, 1024], BF16, name="lq%d" % s) for s in range(2)]
         ys = [keep.tile([P, 512], F32, name="ys%d" % s) for s in range(2)]
         hx = [keep.tile([P, NHE * 1024], BF16, name="hx%d" % s) for s in range(2)]
         le = [keep.tile([P, NCHIP * 1024], BF16, name="le%d" % s) for s in range(2)]
@@ -61,11 +62,11 @@ def tile_qriaffine_kernel(tc, layer1, layer2, layer3, h1, h2, h3, W, out):
         live = {}
 
         def load_x(s):
-            nc.scalar.dma_start(
+            nc.sync.dma_start(
                 out=hr[s][:].rearrange("p (n f) -> p n f", n=NB),
                 in_=(h1, h2)[s].rearrange("n (x t) a -> x n (t a)", t=2),
             )
-            nc.scalar.dma_start(
+            nc.sync.dma_start(
                 out=lr[s][:].rearrange("p (n f) -> p n f", n=NB)[:, :, 0:62],
                 in_=(layer1, layer2)[s].rearrange("n (x t) a -> x n (t a)", t=2),
             )
@@ -79,8 +80,8 @@ def tile_qriaffine_kernel(tc, layer1, layer2, layer3, h1, h2, h3, W, out):
         def constants():
             make_identity(nc, ident[:])
             make_identity(nc, identb[:])
-            nc.gpsimd.memset(ld[0][:], 1.0)
-            nc.gpsimd.memset(ld[1][:], 1.0)
+            nc.vector.memset(ld[0][:], 1.0)
+            nc.vector.memset(ld[1][:], 1.0)
             nc.vector.tensor_copy(
                 out=selh[:].rearrange("p (k a c) -> p k a c", k=16, a=16, c=8),
                 in_=identb[:].rearrange("p (c k) -> p k c", c=8, k=16).unsqueeze(2).to_broadcast([P, 16, 16, 8]),
@@ -116,10 +117,17 @@ def tile_qriaffine_kernel(tc, layer1, layer2, layer3, h1, h2, h3, W, out):
                 .to_broadcast([P, NB, 2, 31, 2]),
             )
 
+        def permute_l(s, engine):
+            copy_on(
+                engine,
+                lq[s][:].bitcast(F32).rearrange("p (j a r) -> p j a r", j=4, a=16),
+                ld[s][:].bitcast(F32).rearrange("p (j r a) -> p j a r", j=4, a=16),
+            )
+
         def park_l(s, engine):
             yps = ps_1.tile([P, 512], F32, name="acc")
             for j in range(4):
-                nc.tensor.transpose(yps[:, P * j : P * j + P], ld[s][:].bitcast(F32)[:, P * j : P * j + P], ident[:])
+                nc.tensor.transpose(yps[:, P * j : P * j + P], lq[s][:].bitcast(F32)[:, P * j : P * j + P], ident[:])
             copy_on(engine, ys[s][:], yps[:])
             nc.gpsimd.dma_start(
                 out=out[NB - 2 + s].rearrange("(j h) (q x) -> (h q) j x", j=4, q=2),
@@ -131,8 +139,8 @@ def tile_qriaffine_kernel(tc, layer1, layer2, layer3, h1, h2, h3, W, out):
                 nc.sync.dma_start(
                     out=ldd[s][:]
                     .bitcast(F32)[c8:P:8, 512 * (n0 - NCHIP) : 512 * (n1 - NCHIP)]
-                    .rearrange("p (r x) -> p r x", x=P),
-                    in_=out[NB - 2 + s].rearrange("(r h) (q x) -> (h q) r x", h=8, q=2)[:, 4 * n0 : 4 * n1, :],
+                    .rearrange("p (j f) -> p j f", f=1024),
+                    in_=out[NB - 2 + s].rearrange("(j a h) w -> a j (h w)", j=4, a=16)[:, n0 // 2 : n1 // 2, :],
                 )
 
         def spread_l(n, s, engine):
@@ -310,19 +318,20 @@ def tile_qriaffine_kernel(tc, layer1, layer2, layer3, h1, h2, h3, W, out):
             select_h(0, s)
             prepare_l(s)
             spread_l(0, s, V)
+            permute_l(s, A)
             flip_l(0, s, A)
             flip_h(s, A)
             park_l(s, A)
+        if NCHIP < 4:
+            for s in range(2):
+                fetch_l(s, NCHIP, 4)
         for s in range(2):
-            fetch_l(s, NCHIP, 4)
-        for s in range(2):
-            fetch_l(s, 4, NB)
+            fetch_l(s, max(4, NCHIP), NB)
         multiply(0, 0)
         multiply(0, 1)
-        for n in range(1, NCHIP):
-            for s in range(2):
-                spread_l(n, s, A)
-                flip_l(n, s, A)
+        for s in range(2):
+            spread_l(1, s, A)
+            flip_l(1, s, A)
         quantise(0, 0)
         quantise(0, 1)
         select_h(1, 0)
@@ -332,8 +341,8 @@ def tile_qriaffine_kernel(tc, layer1, layer2, layer3, h1, h2, h3, W, out):
         multiply(1, 0)
         select_h(2, 0)
         quantise_w(0, 0)
-        quantise_w(0, 1)
         regroup_w(1, 0, V)
+        quantise_w(0, 1)
         regroup_w(1, 1, V, 0, WSPLIT)
         regroup_w(1, 1, A, WSPLIT, 4)
         quantise_w(1, 0)
@@ -343,6 +352,10 @@ def tile_qriaffine_kernel(tc, layer1, layer2, layer3, h1, h2, h3, W, out):
         quantise(1, 1)
         for r in range(1, NB + 2):
             n = r - 1
+            if r + 1 < NCHIP:
+                for s in range(2):
+                    spread_l(r + 1, s, A)
+                    flip_l(r + 1, s, A)
             if 2 <= r < NB:
                 multiply(r, 0)
             if 0 <= n - 1:

@@ -49,8 +49,8 @@ def tile_qriaffine_kernel(tc, layer1, layer2, layer3, h1, h2, h3, W, out):
         ld = [keep.tile([P, 1024], BF16, name="ld%d" % s) for s in range(2)]
         hq = [keep.tile([P, 512], BF16, name="hq%d" % s) for s in range(2)]
         zs = [keep.tile([P, 256], F32, name="zs%d" % s) for s in range(2)]
-        lq = [keep.tile([P, 1024], BF16, name="lq%d" % s) for s in range(2)]
-        ys = [keep.tile([P, 512], F32, name="ys%d" % s) for s in range(2)]
+        lq = [keep.tile([P, (NB - NCHIP) * 256], BF16, name="lq%d" % s) for s in range(2)]
+        ys = [keep.tile([P, (NB - NCHIP) * P], F32, name="ys%d" % s) for s in range(2)]
         hx = [keep.tile([P, NHE * 1024], BF16, name="hx%d" % s) for s in range(2)]
         le = [keep.tile([P, NCHIP * 1024], BF16, name="le%d" % s) for s in range(2)]
         ldd = [keep.tile([P, (NB - NCHIP) * 1024], BF16, name="ldd%d" % s) for s in range(2)]
@@ -118,29 +118,39 @@ def tile_qriaffine_kernel(tc, layer1, layer2, layer3, h1, h2, h3, W, out):
             )
 
         def permute_l(s, engine):
-            copy_on(
-                engine,
-                lq[s][:].bitcast(F32).rearrange("p (j a r) -> p j a r", j=4, a=16),
-                ld[s][:].bitcast(F32).rearrange("p (j r a) -> p j a r", j=4, a=16),
-            )
+            for rep in range(2):
+                copy_on(
+                    engine,
+                    lq[s][:].bitcast(F32).rearrange("p (n a c r) -> p n a c r", a=16, c=2, r=4)[:, :, :, rep, :],
+                    ld[s][:].bitcast(F32)[:, 64 * NCHIP : 512].rearrange("p (n r a) -> p n a r", r=4, a=16),
+                )
+
+        def parked(s):
+            words = (NB - NCHIP) * P * P
+            base = NB * 65536 - (2 - s) * words
+            return out.rearrange("n i j -> (n i j)")[base : base + words]
 
         def park_l(s, engine):
-            yps = ps_1.tile([P, 512], F32, name="acc")
-            for j in range(4):
-                nc.tensor.transpose(yps[:, P * j : P * j + P], lq[s][:].bitcast(F32)[:, P * j : P * j + P], ident[:])
-            copy_on(engine, ys[s][:], yps[:])
+            for lo in range(0, NB - NCHIP, 4):
+                hi = min(lo + 4, NB - NCHIP)
+                yps = ps_1.tile([P, 512], F32, name="acc")
+                for n in range(lo, hi):
+                    nc.tensor.transpose(
+                        yps[:, P * (n - lo) : P * (n - lo) + P], lq[s][:].bitcast(F32)[:, P * n : P * n + P], ident[:]
+                    )
+                copy_on(engine, ys[s][:, P * lo : P * hi], yps[:, 0 : P * (hi - lo)])
             nc.gpsimd.dma_start(
-                out=out[NB - 2 + s].rearrange("(j h) (q x) -> (h q) j x", j=4, q=2),
-                in_=ys[s][:].rearrange("p (j x) -> p j x", j=4),
+                out=parked(s).rearrange("(n m x) -> m n x", m=P, x=P),
+                in_=ys[s][:].rearrange("p (n x) -> p n x", x=P),
             )
 
         def fetch_l(s, n0, n1):
-            for c8 in range(8):
+            for o in range(4):
                 nc.sync.dma_start(
                     out=ldd[s][:]
-                    .bitcast(F32)[c8:P:8, 512 * (n0 - NCHIP) : 512 * (n1 - NCHIP)]
-                    .rearrange("p (j f) -> p j f", f=1024),
-                    in_=out[NB - 2 + s].rearrange("(j a h) w -> a j (h w)", j=4, a=16)[:, n0 // 2 : n1 // 2, :],
+                    .bitcast(F32)[o:P:4, 512 * (n0 - NCHIP) : 512 * (n1 - NCHIP)]
+                    .rearrange("p (n f) -> p n f", f=512),
+                    in_=parked(s).rearrange("(n i f) -> i n f", i=32, f=512)[:, n0 - NCHIP : n1 - NCHIP, :],
                 )
 
         def spread_l(n, s, engine):
@@ -309,7 +319,7 @@ def tile_qriaffine_kernel(tc, layer1, layer2, layer3, h1, h2, h3, W, out):
         load_x(0)
         load_x(1)
         for g in range(2):
-            for c8 in range(8):
+            for c8 in (0, 4, 1, 5, 2, 6, 3, 7):
                 load_w(g, c8)
         constants()
         for s in range(2):

@@ -20,7 +20,8 @@ A = "scalar"
 PINNED = True
 NCHIP = 2
 NHE = 1
-WSPLIT = 2
+WSPLIT = 1
+HBUFS = 4
 
 
 def tile_qriaffine_kernel(tc, layer1, layer2, layer3, h1, h2, h3, W, out):
@@ -28,8 +29,8 @@ def tile_qriaffine_kernel(tc, layer1, layer2, layer3, h1, h2, h3, W, out):
     with ExitStack() as ctx:
         keep = ctx.enter_context(tc.tile_pool(name="keep", bufs=1))
         work = ctx.enter_context(tc.tile_pool(name="work", bufs=3))
-        ps_h = ctx.enter_context(tc.psum_pool(name="ps_h", bufs=2))
-        ps_1 = ctx.enter_context(tc.psum_pool(name="ps_1", bufs=5))
+        ps_h = ctx.enter_context(tc.psum_pool(name="ps_h", bufs=HBUFS))
+        ps_1 = ctx.enter_context(tc.psum_pool(name="ps_1", bufs=7 - HBUFS))
         ps_2 = ctx.enter_context(tc.psum_pool(name="ps_2", bufs=1))
         if PINNED:
             ctx.enter_context(tc.manual_schedule())
@@ -322,34 +323,44 @@ def tile_qriaffine_kernel(tc, layer1, layer2, layer3, h1, h2, h3, W, out):
             for c8 in (0, 4, 1, 5, 2, 6, 3, 7):
                 load_w(g, c8)
         constants()
-        for s in range(2):
-            permute_h(s)
-            spread_h(0, s)
-            select_h(0, s)
-            prepare_l(s)
-            spread_l(0, s, V)
-            permute_l(s, A)
-            flip_l(0, s, A)
-            flip_h(s, A)
-            park_l(s, A)
-        if NCHIP < 4:
-            for s in range(2):
-                fetch_l(s, NCHIP, 4)
-        for s in range(2):
-            fetch_l(s, max(4, NCHIP), NB)
+        permute_h(0)
+        spread_h(0, 0)
+        select_h(0, 0)
+        prepare_l(0)
+        spread_l(0, 0, V)
+        permute_l(0, A)
+        flip_l(0, 0, A)
+        flip_h(0, A)
+        permute_h(1)
+        spread_h(0, 1)
+        select_h(0, 1)
+        prepare_l(1)
+        spread_l(0, 1, V)
+        park_l(0, A)
+        flip_l(0, 1, A)
         multiply(0, 0)
+        flip_h(1, A)
+        spread_l(1, 0, A)
         multiply(0, 1)
+        permute_l(1, A)
+        flip_l(1, 0, A)
+        spread_l(1, 1, A)
+        park_l(1, A)
+        flip_l(1, 1, A)
         for s in range(2):
-            spread_l(1, s, A)
-            flip_l(1, s, A)
+            fetch_l(s, NCHIP, 4)
+        for s in range(2):
+            fetch_l(s, 4, NB)
         quantise(0, 0)
         quantise(0, 1)
         select_h(1, 0)
         select_h(1, 1)
+        select_h(2, 0)
+        select_h(2, 1)
         regroup_w(0, 0, V)
         regroup_w(0, 1, A)
         multiply(1, 0)
-        select_h(2, 0)
+        select_h(3, 0)
         quantise_w(0, 0)
         regroup_w(1, 0, V)
         quantise_w(0, 1)
@@ -362,10 +373,6 @@ def tile_qriaffine_kernel(tc, layer1, layer2, layer3, h1, h2, h3, W, out):
         quantise(1, 1)
         for r in range(1, NB + 2):
             n = r - 1
-            if r + 1 < NCHIP:
-                for s in range(2):
-                    spread_l(r + 1, s, A)
-                    flip_l(r + 1, s, A)
             if 2 <= r < NB:
                 multiply(r, 0)
             if 0 <= n - 1:
@@ -381,7 +388,7 @@ def tile_qriaffine_kernel(tc, layer1, layer2, layer3, h1, h2, h3, W, out):
             if 0 <= n - 1:
                 second_product(n - 1)
                 deliver(n - 1, A)
-            if r + 1 < NB:
+            if r + 2 < NB:
                 if r > 1:
-                    select_h(r + 1, 0)
-                select_h(r + 1, 1)
+                    select_h(r + 2, 0)
+                select_h(r + 2, 1)

@@ -120,11 +120,12 @@ def tile_qriaffine_kernel(tc, layer1, layer2, layer3, h1, h2, h3, W, out):
 
         def permute_l(s, engine):
             for rep in range(2):
-                copy_on(
-                    engine,
-                    lq[s][:].bitcast(F32).rearrange("p (n a c r) -> p n a c r", a=16, c=2, r=4)[:, :, :, rep, :],
-                    ld[s][:].bitcast(F32)[:, 64 * NCHIP : 512].rearrange("p (n r a) -> p n a r", r=4, a=16),
-                )
+                for g in range(2):
+                    copy_on(
+                        engine,
+                        lq[s][:].bitcast(F32).rearrange("p (n a c g t) -> p n a c g t", a=16, c=2, g=2, t=2)[:, :, :, rep, g, :],
+                        ld[s][:].bitcast(F32)[:, 64 * NCHIP : 512].rearrange("p (n t g a) -> p n a g t", t=2, g=2, a=16)[:, :, :, g, :],
+                    )
 
         def parked(s):
             words = (NB - NCHIP) * P * P
@@ -163,8 +164,11 @@ def tile_qriaffine_kernel(tc, layer1, layer2, layer3, h1, h2, h3, W, out):
 
         def flip_l(n, s, engine):
             lps = ps_1.tile([P, 512], F32, name="acc")
-            for o in range(0, 512, P):
-                nc.tensor.transpose(lps[:, o : o + P], le[s][:].bitcast(F32)[:, 512 * n + o : 512 * n + o + P], ident[:])
+            for g in range(2):
+                for t in range(2):
+                    o = (2 * g + t) * P
+                    i = 512 * n + 256 * t + P * g
+                    nc.tensor.transpose(lps[:, o : o + P], le[s][:].bitcast(F32)[:, i : i + P], ident[:])
             ls = work.tile([P, 1024], BF16, name="ls", bufs=2 * NCHIP)
             copy_on(engine, ls[:].bitcast(F32), lps[:])
             live["ls", n, s] = ls
@@ -208,23 +212,23 @@ def tile_qriaffine_kernel(tc, layer1, layer2, layer3, h1, h2, h3, W, out):
                 for t in range(2):
                     for g in range(2):
                         nc.vector.tensor_tensor(
-                            out=grouped[:].rearrange("p (t g x u e) -> p t g x u e", t=2, g=2, u=2, e=2)[:, t, g],
+                            out=grouped[:].rearrange("p (g t x u e) -> p g t x u e", t=2, g=2, u=2, e=2)[:, g, t],
                             in0=live["hps", n, s][:]
                             .bitcast(BF16)
                             .rearrange("p (t u x e) -> p t x u e", t=2, u=2, e=2)[:, t],
-                            in1=lsrc.rearrange("p (t g x e) -> p t g x e", t=2, g=2, e=2)[:, t, g]
+                            in1=lsrc.rearrange("p (g t x e) -> p g t x e", t=2, g=2, e=2)[:, g, t]
                             .unsqueeze(2)
                             .to_broadcast([P, P, 2, 2]),
                             op=MULT,
                         )
                 return
             nc.vector.tensor_tensor(
-                out=grouped[:].rearrange("p (t g x u e) -> p t g x u e", t=2, g=2, u=2, e=2),
+                out=grouped[:].rearrange("p (g w u e) -> p g w u e", g=2, u=2, e=2),
                 in0=live["hps", n, s][:]
-                .rearrange("p (t x u e) -> p t x u e", t=2, u=2, e=2)
-                .unsqueeze(2)
-                .to_broadcast([P, 2, 2, P, 2, 2]),
-                in1=lsrc.rearrange("p (t g x e) -> p t g x e", t=2, g=2, e=2).unsqueeze(4).to_broadcast([P, 2, 2, P, 2, 2]),
+                .rearrange("p (w u e) -> p w u e", u=2, e=2)
+                .unsqueeze(1)
+                .to_broadcast([P, 2, 256, 2, 2]),
+                in1=lsrc.rearrange("p (g w e) -> p g w e", g=2, e=2).unsqueeze(3).to_broadcast([P, 2, 256, 2, 2]),
                 op=MULT,
             )
             live["grouped", n, s] = grouped
@@ -261,7 +265,7 @@ def tile_qriaffine_kernel(tc, layer1, layer2, layer3, h1, h2, h3, W, out):
             for tt in range(4):
                 for g in range(2):
                     wo = 1024 * g + 512 * g2 + P * tt
-                    po = 512 * n + 256 * t + P * g
+                    po = 512 * n + 256 * g + P * t
                     nc.tensor.matmul_mx(
                         out=acc[:, P * tt : P * tt + P],
                         lhsT=wc[:, wo : wo + P].bitcast(FP8X4),
@@ -292,20 +296,19 @@ def tile_qriaffine_kernel(tc, layer1, layer2, layer3, h1, h2, h3, W, out):
 
         def second_product(n):
             res = ps_2.tile([P, 512], F32, name="res")
-            for ti in range(2):
-                for tj in range(2):
-                    for g2 in range(2):
-                        qo = 256 * g2 + P * ti
-                        ro = 512 * n + 256 * tj + P * g2
-                        nc.tensor.matmul_mx(
-                            out=res[:, 256 * ti + P * tj : 256 * ti + P * tj + P],
-                            lhsT=live["qc", n][:, qo : qo + P].bitcast(FP8X4),
-                            lhsT_scale=live["qs", n][:, qo : qo + P],
-                            rhs=codes[1][:, ro : ro + P].bitcast(FP8X4),
-                            rhs_scale=planes[1][:, ro : ro + P],
-                            start=(g2 == 0),
-                            stop=(g2 == 1),
-                        )
+            for t in range(2):
+                for g2 in range(2):
+                    qo = 256 * g2 + P * t
+                    ro = 512 * n + 256 * g2
+                    nc.tensor.matmul_mx(
+                        out=res[:, 256 * t : 256 * t + 256],
+                        lhsT=live["qc", n][:, qo : qo + P].bitcast(FP8X4),
+                        lhsT_scale=live["qs", n][:, qo : qo + P],
+                        rhs=codes[1][:, ro : ro + 256].bitcast(FP8X4),
+                        rhs_scale=planes[1][:, ro : ro + 256],
+                        start=(g2 == 0),
+                        stop=(g2 == 1),
+                    )
             live["res", n] = res
 
         def deliver(n, engine):
@@ -317,6 +320,18 @@ def tile_qriaffine_kernel(tc, layer1, layer2, layer3, h1, h2, h3, W, out):
             )
             nc.sync.dma_start(out=out[n].rearrange("(x t) j -> x (t j)", t=2), in_=ob[:])
 
+        order = [(0, 0), (0, 1), (1, 0), (1, 1), (2, 0)]
+        for n in range(3, NB):
+            order.extend([(n, 0), (n - 1, 1)])
+        order.append((NB - 1, 1))
+        selected = []
+
+        def prefetch(limit):
+            while len(selected) < min(limit, len(order)):
+                n, s = order[len(selected)]
+                select_h(n, s)
+                selected.append((n, s))
+
         load_x(0)
         load_x(1)
         for g in range(2):
@@ -325,7 +340,7 @@ def tile_qriaffine_kernel(tc, layer1, layer2, layer3, h1, h2, h3, W, out):
         constants()
         permute_h(0)
         spread_h(0, 0)
-        select_h(0, 0)
+        prefetch(1)
         prepare_l(0)
         spread_l(0, 0, V)
         permute_l(0, A)
@@ -333,7 +348,7 @@ def tile_qriaffine_kernel(tc, layer1, layer2, layer3, h1, h2, h3, W, out):
         flip_h(0, A)
         permute_h(1)
         spread_h(0, 1)
-        select_h(0, 1)
+        prefetch(2)
         prepare_l(1)
         spread_l(0, 1, V)
         park_l(0, A)
@@ -353,42 +368,38 @@ def tile_qriaffine_kernel(tc, layer1, layer2, layer3, h1, h2, h3, W, out):
             fetch_l(s, 4, NB)
         quantise(0, 0)
         quantise(0, 1)
-        select_h(1, 0)
-        select_h(1, 1)
-        select_h(2, 0)
-        select_h(2, 1)
+        prefetch(HBUFS + 2)
         regroup_w(0, 0, V)
         regroup_w(0, 1, A)
         multiply(1, 0)
-        select_h(3, 0)
+        prefetch(HBUFS + 3)
         quantise_w(0, 0)
         regroup_w(1, 0, V)
         quantise_w(0, 1)
+        quantise_w(1, 0)
         regroup_w(1, 1, V, 0, WSPLIT)
         regroup_w(1, 1, A, WSPLIT, 4)
-        quantise_w(1, 0)
         quantise_w(1, 1)
         quantise(1, 0)
         multiply(1, 1)
-        quantise(1, 1)
-        for r in range(1, NB + 2):
-            n = r - 1
-            if 2 <= r < NB:
+        for b in range(4):
+            first_product(0, b)
+            fetch_q(0, b, A)
+        prefetch(HBUFS + 4)
+        for r in range(2, NB + 2):
+            if r < NB:
                 multiply(r, 0)
-            if 0 <= n - 1:
-                quantise_q(n - 1)
-            if 2 <= r < NB:
-                multiply(r, 1)
+            if r >= 3:
+                quantise(r - 2, 1)
+            quantise_q(r - 2)
+            if r < NB:
                 quantise(r, 0)
-                quantise(r, 1)
-            if n < NB:
+            if 3 <= r <= NB:
+                multiply(r - 1, 1)
+            if r <= NB:
                 for b in range(4):
-                    first_product(n, b)
-                    fetch_q(n, b, A)
-            if 0 <= n - 1:
-                second_product(n - 1)
-                deliver(n - 1, A)
-            if r + 2 < NB:
-                if r > 1:
-                    select_h(r + 2, 0)
-                select_h(r + 2, 1)
+                    first_product(r - 1, b)
+                    fetch_q(r - 1, b, A)
+            second_product(r - 2)
+            deliver(r - 2, A)
+            prefetch(HBUFS + 2 * r + (1 if r >= 3 else 1))

@@ -30,8 +30,7 @@ def tile_qriaffine_kernel(tc, layer1, layer2, layer3, h1, h2, h3, W, out):
         keep = ctx.enter_context(tc.tile_pool(name="keep", bufs=1))
         work = ctx.enter_context(tc.tile_pool(name="work", bufs=3))
         ps_h = ctx.enter_context(tc.psum_pool(name="ps_h", bufs=HBUFS))
-        ps_1 = ctx.enter_context(tc.psum_pool(name="ps_1", bufs=7 - HBUFS))
-        ps_2 = ctx.enter_context(tc.psum_pool(name="ps_2", bufs=1))
+        ps_1 = ctx.enter_context(tc.psum_pool(name="ps_1", bufs=8 - HBUFS))
         if PINNED:
             ctx.enter_context(tc.manual_schedule())
 
@@ -119,6 +118,17 @@ def tile_qriaffine_kernel(tc, layer1, layer2, layer3, h1, h2, h3, W, out):
             )
 
         def permute_l(s, engine):
+            if engine == V:
+                for g in range(2):
+                    nc.vector.tensor_copy(
+                        out=lq[s][:].bitcast(F32).rearrange("p (n a c g t) -> p n a c g t", a=16, c=2, g=2, t=2)[:, :, :, :, g, :],
+                        in_=ld[s][:]
+                        .bitcast(F32)[:, 64 * NCHIP : 512]
+                        .rearrange("p (n t g a) -> p n a g t", t=2, g=2, a=16)[:, :, :, g, :]
+                        .unsqueeze(3)
+                        .to_broadcast([P, NB - NCHIP, 16, 2, 2]),
+                    )
+                return
             for rep in range(2):
                 for g in range(2):
                     copy_on(
@@ -295,7 +305,7 @@ def tile_qriaffine_kernel(tc, layer1, layer2, layer3, h1, h2, h3, W, out):
             live["qs", n] = qs
 
         def second_product(n):
-            res = ps_2.tile([P, 512], F32, name="res")
+            res = ps_1.tile([P, 512], F32, name="acc")
             for t in range(2):
                 for g2 in range(2):
                     qo = 256 * g2 + P * t
@@ -355,11 +365,11 @@ def tile_qriaffine_kernel(tc, layer1, layer2, layer3, h1, h2, h3, W, out):
         flip_l(0, 1, A)
         multiply(0, 0)
         flip_h(1, A)
-        spread_l(1, 0, A)
+        spread_l(1, 0, V)
         multiply(0, 1)
         permute_l(1, A)
         flip_l(1, 0, A)
-        spread_l(1, 1, A)
+        spread_l(1, 1, V)
         park_l(1, A)
         flip_l(1, 1, A)
         for s in range(2):

@@ -47,7 +47,7 @@ def tile_qriaffine_kernel(tc, layer1, layer2, layer3, h1, h2, h3, W, out):
         identb = keep.tile([P, P], BF16, name="identb")
         selh = keep.tile([P, 2048], BF16, name="selh")
         ld = [keep.tile([P, 1024], BF16, name="ld%d" % s) for s in range(2)]
-        hq = [keep.tile([P, 512], BF16, name="hq%d" % s) for s in range(2)]
+        hq = keep.tile([P, 512], BF16, name="hq")
         zs = [keep.tile([P, 256], F32, name="zs%d" % s) for s in range(2)]
         lq = [keep.tile([P, (NB - NCHIP) * 256], BF16, name="lq%d" % s) for s in range(2)]
         ys = [keep.tile([P, (NB - NCHIP) * P], F32, name="ys%d" % s) for s in range(2)]
@@ -79,28 +79,33 @@ def tile_qriaffine_kernel(tc, layer1, layer2, layer3, h1, h2, h3, W, out):
 
         def constants():
             make_identity(nc, ident[:])
-            make_identity(nc, identb[:])
-            nc.vector.memset(ld[0][:], 1.0)
-            nc.vector.memset(ld[1][:], 1.0)
+            for s in range(2):
+                nc.vector.memset(ld[s][:].rearrange("p (q a e) -> p q a e", a=32, e=2)[:, :, 31, :], 1.0)
+
+        def selectors():
+            nc.vector.tensor_copy(out=identb[:], in_=ident[:])
             nc.vector.tensor_copy(
                 out=selh[:].rearrange("p (k a c) -> p k a c", k=16, a=16, c=8),
-                in_=identb[:].rearrange("p (c k) -> p k c", c=8, k=16).unsqueeze(2).to_broadcast([P, 16, 16, 8]),
+                in_=identb[:].rearrange("p (k c) -> p k c", c=8, k=16).unsqueeze(2).to_broadcast([P, 16, 16, 8]),
             )
 
-        def permute_h(s):
+        def h_words(s):
+            if s == 0:
+                return hr[0][:].bitcast(F32).rearrange("p (k c u) -> p k u c", c=8, u=2)
+            return hq[:].bitcast(F32).rearrange("p (u k c) -> p k u c", u=2, c=8)
+
+        def permute_h():
             for u in range(2):
-                if s == 0:
-                    src = hr[0][:].rearrange("p (k c u e) -> p u c k e", c=8, u=2, e=2)[:, u]
-                else:
-                    src = hr[1][:].rearrange("p (k u e d) -> p u d k e", u=2, e=2, d=8)[:, u]
                 nc.vector.tensor_copy(
-                    out=hq[s][:].rearrange("p (u c k e) -> p u c k e", u=2, c=8, k=16, e=2)[:, u], in_=src
+                    out=hq[:].rearrange("p (u k d e) -> p u k d e", u=2, d=8, k=16, e=2)[:, u],
+                    in_=hr[1][:].rearrange("p (k u e d) -> p u k d e", u=2, e=2, d=8)[:, u],
                 )
 
         def flip_h(s, engine):
             zps = ps_1.tile([P, 512], F32, name="acc")
             for u in range(2):
-                nc.tensor.transpose(zps[:, P * u : P * u + P], hq[s][:].bitcast(F32)[:, P * u : P * u + P], ident[:])
+                words = hr[0][:].bitcast(F32)[:, u:256:2] if s == 0 else hq[:].bitcast(F32)[:, P * u : P * u + P]
+                nc.tensor.transpose(zps[:, P * u : P * u + P], words, ident[:])
             copy_on(
                 engine,
                 zs[s][:].rearrange("p (x u) -> p x u", u=2),
@@ -186,9 +191,7 @@ def tile_qriaffine_kernel(tc, layer1, layer2, layer3, h1, h2, h3, W, out):
         def spread_h(n, s):
             nc.vector.tensor_copy(
                 out=hx[s][:].bitcast(F32)[:, 512 * n : 512 * n + 512].rearrange("p (t u a c) -> p t u a c", t=2, u=2, a=16),
-                in_=hq[s][:]
-                .bitcast(F32)
-                .rearrange("p (u c k) -> p k u c", u=2, c=8)[:, 2 * n : 2 * n + 2]
+                in_=h_words(s)[:, 2 * n : 2 * n + 2]
                 .unsqueeze(3)
                 .to_broadcast([P, 2, 2, 16, 8]),
             )
@@ -348,7 +351,6 @@ def tile_qriaffine_kernel(tc, layer1, layer2, layer3, h1, h2, h3, W, out):
             for c8 in (0, 4, 1, 5, 2, 6, 3, 7):
                 load_w(g, c8)
         constants()
-        permute_h(0)
         spread_h(0, 0)
         prefetch(1)
         prepare_l(0)
@@ -356,11 +358,12 @@ def tile_qriaffine_kernel(tc, layer1, layer2, layer3, h1, h2, h3, W, out):
         permute_l(0, A)
         flip_l(0, 0, A)
         flip_h(0, A)
-        permute_h(1)
+        permute_h()
         spread_h(0, 1)
         prefetch(2)
         prepare_l(1)
         spread_l(0, 1, V)
+        selectors()
         park_l(0, A)
         flip_l(0, 1, A)
         multiply(0, 0)

@@ -255,9 +255,9 @@ def tile_qriaffine_kernel(tc, layer1, layer2, layer3, h1, h2, h3, W, out):
 
         def regroup_w(g, g2, engine, t0=0, t1=4):
             dst = wg[:, 4096 * g + 2048 * g2 : 4096 * g + 2048 * g2 + 2048].rearrange(
-                "p (t b d j) -> p t b j d", t=4, b=16, d=8, j=4
+                "p (t b d j) -> p t b d j", t=4, b=16, d=8, j=4
             )
-            src = wr[g][:, 2048 * g2 : 2048 * g2 + 2048].rearrange("p (b j t d) -> p t b j d", b=16, j=4, t=4, d=8)
+            src = wr[g][:, 2048 * g2 : 2048 * g2 + 2048].rearrange("p (b j t d) -> p t b d j", b=16, j=4, t=4, d=8)
             if engine == V:
                 nc.vector.tensor_copy(out=dst[:, t0:t1], in_=src[:, t0:t1])
             else:
@@ -351,6 +351,7 @@ def tile_qriaffine_kernel(tc, layer1, layer2, layer3, h1, h2, h3, W, out):
             for c8 in (0, 4, 1, 5, 2, 6, 3, 7):
                 load_w(g, c8)
         constants()
+        selectors()
         spread_h(0, 0)
         prefetch(1)
         prepare_l(0)
@@ -363,7 +364,6 @@ def tile_qriaffine_kernel(tc, layer1, layer2, layer3, h1, h2, h3, W, out):
         prefetch(2)
         prepare_l(1)
         spread_l(0, 1, V)
-        selectors()
         park_l(0, A)
         flip_l(0, 1, A)
         multiply(0, 0)

@@ -124,14 +124,10 @@ def tile_qriaffine_kernel(tc, layer1, layer2, layer3, h1, h2, h3, W, out):
 
         def permute_l(s, engine):
             if engine == V:
-                for g in range(2):
+                for rep in range(2):
                     nc.vector.tensor_copy(
-                        out=lq[s][:].bitcast(F32).rearrange("p (n a c g t) -> p n a c g t", a=16, c=2, g=2, t=2)[:, :, :, :, g, :],
-                        in_=ld[s][:]
-                        .bitcast(F32)[:, 64 * NCHIP : 512]
-                        .rearrange("p (n t g a) -> p n a g t", t=2, g=2, a=16)[:, :, :, g, :]
-                        .unsqueeze(3)
-                        .to_broadcast([P, NB - NCHIP, 16, 2, 2]),
+                        out=lq[s][:].bitcast(F32).rearrange("p (n a c g t) -> p n a c g t", a=16, c=2, g=2, t=2)[:, :, :, rep],
+                        in_=ld[s][:].bitcast(F32)[:, 64 * NCHIP : 512].rearrange("p (n t g a) -> p n a g t", t=2, g=2, a=16),
                     )
                 return
             for rep in range(2):
@@ -356,7 +352,7 @@ def tile_qriaffine_kernel(tc, layer1, layer2, layer3, h1, h2, h3, W, out):
         prefetch(1)
         prepare_l(0)
         spread_l(0, 0, V)
-        permute_l(0, A)
+        permute_l(0, V)
         flip_l(0, 0, A)
         flip_h(0, A)
         permute_h()
@@ -368,9 +364,10 @@ def tile_qriaffine_kernel(tc, layer1, layer2, layer3, h1, h2, h3, W, out):
         flip_l(0, 1, A)
         multiply(0, 0)
         flip_h(1, A)
+        prefetch(4)
         spread_l(1, 0, V)
         multiply(0, 1)
-        permute_l(1, A)
+        permute_l(1, V)
         flip_l(1, 0, A)
         spread_l(1, 1, V)
         park_l(1, A)

@@ -20,7 +20,6 @@ A = "scalar"
 PINNED = True
 NCHIP = 2
 NHE = 1
-WSPLIT = 1
 HBUFS = 4
 
 
@@ -269,7 +268,7 @@ def tile_qriaffine_kernel(tc, layer1, layer2, layer3, h1, h2, h3, W, out):
             )
 
         def first_product(n, b):
-            g2, t = divmod(b, 2)
+            t, g2 = divmod(b, 2)
             acc = ps_1.tile([P, 512], F32, name="acc")
             for tt in range(4):
                 for g in range(2):
@@ -296,29 +295,50 @@ def tile_qriaffine_kernel(tc, layer1, layer2, layer3, h1, h2, h3, W, out):
                 live["acc", n, b][:].rearrange("p (k w) -> p w k", k=4),
             )
 
-        def quantise_q(n):
-            qc = work.tile([P, 512], U32, name="qc", align_bytes=64)
-            qs = work.tile([P, 512], U8, name="qs", align_bytes=64)
-            nc.vector.quantize_mx(out=qc[:].bitcast(FP8X4), scales=qs[:], in_=live["qg", n][:])
-            live["qc", n] = qc
-            live["qs", n] = qs
+        def quantise_q(n, halves=(0, 1)):
+            if ("qc", n) not in live:
+                qc = work.tile([P, 512], U32, name="qc", align_bytes=64)
+                qs = work.tile([P, 512], U8, name="qs", align_bytes=64)
+                live["qc", n] = qc
+                live["qs", n] = qs
+            lo, hi = 256 * halves[0], 256 * halves[-1] + 256
+            nc.vector.quantize_mx(
+                out=live["qc", n][:, lo:hi].bitcast(FP8X4),
+                scales=live["qs", n][:, lo:hi],
+                in_=live["qg", n][:, 4 * lo : 4 * hi],
+            )
+
+        def second_passes(n, t, dst):
+            for g2 in range(2):
+                qo = 256 * t + P * g2
+                ro = 512 * n + 256 * g2
+                nc.tensor.matmul_mx(
+                    out=dst,
+                    lhsT=live["qc", n][:, qo : qo + P].bitcast(FP8X4),
+                    lhsT_scale=live["qs", n][:, qo : qo + P],
+                    rhs=codes[1][:, ro : ro + 256].bitcast(FP8X4),
+                    rhs_scale=planes[1][:, ro : ro + 256],
+                    start=(g2 == 0),
+                    stop=(g2 == 1),
+                )
 
         def second_product(n):
             res = ps_1.tile([P, 512], F32, name="acc")
             for t in range(2):
-                for g2 in range(2):
-                    qo = 256 * g2 + P * t
-                    ro = 512 * n + 256 * g2
-                    nc.tensor.matmul_mx(
-                        out=res[:, 256 * t : 256 * t + 256],
-                        lhsT=live["qc", n][:, qo : qo + P].bitcast(FP8X4),
-                        lhsT_scale=live["qs", n][:, qo : qo + P],
-                        rhs=codes[1][:, ro : ro + 256].bitcast(FP8X4),
-                        rhs_scale=planes[1][:, ro : ro + 256],
-                        start=(g2 == 0),
-                        stop=(g2 == 1),
-                    )
+                second_passes(n, t, res[:, 256 * t : 256 * t + 256])
             live["res", n] = res
+
+        def finish_half(n, t, engine):
+            quantise_q(n, (t,))
+            res = ps_1.tile([P, 512], F32, name="acc")
+            second_passes(n, t, res[:, 0:256])
+            ob = work.tile([P, 512], F32, name="ob")
+            copy_on(
+                engine,
+                ob[:, 0:256].rearrange("p (x s) -> p x s", s=2),
+                res[:, 0:256].rearrange("p (s x) -> p x s", s=2),
+            )
+            nc.sync.dma_start(out=out[n].rearrange("(x t) j -> x t j", t=2)[:, t, :], in_=ob[:, 0:256])
 
         def deliver(n, engine):
             ob = work.tile([P, 512], F32, name="ob")
@@ -365,6 +385,7 @@ def tile_qriaffine_kernel(tc, layer1, layer2, layer3, h1, h2, h3, W, out):
         multiply(0, 0)
         flip_h(1, A)
         prefetch(4)
+        regroup_w(0, 1, A)
         spread_l(1, 0, V)
         multiply(0, 1)
         permute_l(1, V)
@@ -380,28 +401,30 @@ def tile_qriaffine_kernel(tc, layer1, layer2, layer3, h1, h2, h3, W, out):
         quantise(0, 1)
         prefetch(HBUFS + 2)
         regroup_w(0, 0, V)
-        regroup_w(0, 1, A)
-        multiply(1, 0)
-        prefetch(HBUFS + 3)
-        quantise_w(0, 0)
+        regroup_w(1, 1, A)
         regroup_w(1, 0, V)
-        quantise_w(0, 1)
+        quantise_w(0, 0)
         quantise_w(1, 0)
-        regroup_w(1, 1, V, 0, WSPLIT)
-        regroup_w(1, 1, A, WSPLIT, 4)
-        quantise_w(1, 1)
-        quantise(1, 0)
-        multiply(1, 1)
-        for b in range(4):
+        for b in (0, 2):
             first_product(0, b)
             fetch_q(0, b, A)
+        multiply(1, 0)
+        prefetch(HBUFS + 3)
+        quantise_w(0, 1)
+        quantise_w(1, 1)
+        for b in (1, 3):
+            first_product(0, b)
+            fetch_q(0, b, A)
+        quantise(1, 0)
+        multiply(1, 1)
         prefetch(HBUFS + 4)
         for r in range(2, NB + 2):
             if r < NB:
                 multiply(r, 0)
             if r >= 3:
                 quantise(r - 2, 1)
-            quantise_q(r - 2)
+            if r - 2 < NB - 1:
+                quantise_q(r - 2)
             if r < NB:
                 quantise(r, 0)
             if 3 <= r <= NB:
@@ -410,6 +433,10 @@ def tile_qriaffine_kernel(tc, layer1, layer2, layer3, h1, h2, h3, W, out):
                 for b in range(4):
                     first_product(r - 1, b)
                     fetch_q(r - 1, b, A)
-            second_product(r - 2)
-            deliver(r - 2, A)
+            if r - 2 < NB - 1:
+                second_product(r - 2)
+                deliver(r - 2, A)
+            else:
+                finish_half(r - 2, 0, A)
+                finish_half(r - 2, 1, V)
             prefetch(HBUFS + 2 * r + (1 if r >= 3 else 1))

@@ -259,6 +259,12 @@ def tile_qriaffine_kernel(tc, layer1, layer2, layer3, h1, h2, h3, W, out):
                 for t in range(t0, t1):
                     nc.scalar.copy(out=dst[:, t], in_=src[:, t])
 
+        def keep_warm(g, g2, times):
+            for i in range(times):
+                idle = ps_1.tile([P, 512], F32, name="acc")
+                o = 4096 * g + 2048 * g2 + 512 * i
+                nc.tensor.matmul(out=idle[:], lhsT=identb[:], rhs=wg[:, o : o + 512], start=True, stop=True)
+
         def quantise_w(g, g2):
             o = 1024 * g + 512 * g2
             nc.vector.quantize_mx(
@@ -401,8 +407,10 @@ def tile_qriaffine_kernel(tc, layer1, layer2, layer3, h1, h2, h3, W, out):
         quantise(0, 1)
         prefetch(HBUFS + 2)
         regroup_w(0, 0, V)
+        keep_warm(0, 0, 1)
         regroup_w(1, 1, A)
         regroup_w(1, 0, V)
+        keep_warm(1, 0, 2)
         quantise_w(0, 0)
         quantise_w(1, 0)
         for b in (0, 2):

@@ -20,6 +20,7 @@ A = "scalar"
 PINNED = True
 NCHIP = 2
 NHE = 1
+NSEL = 4
 HBUFS = 4
 
 
@@ -44,12 +45,12 @@ def tile_qriaffine_kernel(tc, layer1, layer2, layer3, h1, h2, h3, W, out):
         wr = [keep.tile([P, 4096], BF16, name="wr%d" % g) for g in range(2)]
         ident = keep.tile([P, P], F32, name="ident")
         identb = keep.tile([P, P], BF16, name="identb")
-        selh = keep.tile([P, 2048], BF16, name="selh")
+        selh = keep.tile([P, 2 * NSEL * P], BF16, name="selh")
         ld = [keep.tile([P, 1024], BF16, name="ld%d" % s) for s in range(2)]
-        hq = keep.tile([P, 512], BF16, name="hq")
+        hq = [keep.tile([P, 512], BF16, name="hq%d" % s) for s in range(2)]
+        hh = [keep.tile([P, (NB - NSEL) * 1024], BF16, name="hh%d" % s) for s in range(2)]
         zs = [keep.tile([P, 256], F32, name="zs%d" % s) for s in range(2)]
-        lq = [keep.tile([P, (NB - NCHIP) * 256], BF16, name="lq%d" % s) for s in range(2)]
-        ys = [keep.tile([P, (NB - NCHIP) * P], F32, name="ys%d" % s) for s in range(2)]
+        ys = [keep.tile([P, (NB - NCHIP) * P // 2], F32, name="ys%d" % s) for s in range(2)]
         hx = [keep.tile([P, NHE * 1024], BF16, name="hx%d" % s) for s in range(2)]
         le = [keep.tile([P, NCHIP * 1024], BF16, name="le%d" % s) for s in range(2)]
         ldd = [keep.tile([P, (NB - NCHIP) * 1024], BF16, name="ldd%d" % s) for s in range(2)]
@@ -79,106 +80,116 @@ def tile_qriaffine_kernel(tc, layer1, layer2, layer3, h1, h2, h3, W, out):
         def constants():
             make_identity(nc, ident[:])
             for s in range(2):
-                nc.vector.memset(ld[s][:].rearrange("p (q a e) -> p q a e", a=32, e=2)[:, :, 31, :], 1.0)
+                nc.vector.memset(ld[s][:].rearrange("p (n a g f) -> p n a g f", a=16, g=2, f=4)[:, :, 15, 1, :], 1.0)
 
         def selectors():
             nc.vector.tensor_copy(out=identb[:], in_=ident[:])
-            nc.vector.tensor_copy(
-                out=selh[:].rearrange("p (k a c) -> p k a c", k=16, a=16, c=8),
-                in_=identb[:].rearrange("p (k c) -> p k c", c=8, k=16).unsqueeze(2).to_broadcast([P, 16, 16, 8]),
-            )
+            for t in range(2):
+                nc.vector.tensor_copy(
+                    out=selh[:].rearrange("p (n t a c) -> p t n a c", t=2, a=16, c=8)[:, t],
+                    in_=identb[:]
+                    .rearrange("p (n c t) -> p t n c", c=8, t=2)[:, t, 0:NSEL]
+                    .unsqueeze(2)
+                    .to_broadcast([P, NSEL, 16, 8]),
+                )
 
-        def h_words(s):
+        def permute_h(s):
             if s == 0:
-                return hr[0][:].bitcast(F32).rearrange("p (k c u) -> p k u c", c=8, u=2)
-            return hq[:].bitcast(F32).rearrange("p (u k c) -> p k u c", u=2, c=8)
-
-        def permute_h():
+                nc.vector.tensor_copy(
+                    out=hq[0][:].bitcast(F32).rearrange("p (u n c t) -> p u n c t", u=2, c=8, t=2),
+                    in_=hr[0][:].bitcast(F32).rearrange("p (n t c u) -> p u n c t", u=2, c=8, t=2),
+                )
+                return
             for u in range(2):
                 nc.vector.tensor_copy(
-                    out=hq[:].rearrange("p (u k d e) -> p u k d e", u=2, d=8, k=16, e=2)[:, u],
-                    in_=hr[1][:].rearrange("p (k u e d) -> p u k d e", u=2, e=2, d=8)[:, u],
+                    out=hq[1][:].rearrange("p (u n d t e) -> p u n d t e", u=2, d=8, t=2, e=2)[:, u],
+                    in_=hr[1][:].rearrange("p (n t u e d) -> p u n d t e", u=2, e=2, d=8, t=2)[:, u],
                 )
 
         def flip_h(s, engine):
             zps = ps_1.tile([P, 512], F32, name="acc")
             for u in range(2):
-                words = hr[0][:].bitcast(F32)[:, u:256:2] if s == 0 else hq[:].bitcast(F32)[:, P * u : P * u + P]
-                nc.tensor.transpose(zps[:, P * u : P * u + P], words, ident[:])
+                nc.tensor.transpose(
+                    zps[:, P * u : P * u + P], hq[s][:].bitcast(F32)[:, P * u : P * u + P], ident[:]
+                )
             copy_on(
                 engine,
                 zs[s][:].rearrange("p (x u) -> p x u", u=2),
                 zps[:, 0:256].rearrange("p (u x) -> p x u", u=2),
             )
 
-        def prepare_l(s):
-            nc.vector.tensor_copy(
-                out=ld[s][:].rearrange("p (n t a e) -> p n t a e", t=2, a=32, e=2)[:, :, :, 0:31, :],
-                in_=lr[s][:]
-                .rearrange("p (n f) -> p n f", n=NB)[:, :, 0:62]
-                .rearrange("p n (t a) -> p n t a", t=2)
-                .unsqueeze(4)
-                .to_broadcast([P, NB, 2, 31, 2]),
+        def h_parked(s):
+            words = (NB - NSEL) * 16 * 256
+            base = NB * 65536 - 2 * (NB - NCHIP) * 64 * P - (2 - s) * words
+            return out.rearrange("n i j -> (n i j)")[base : base + words]
+
+        def park_h(s):
+            nc.gpsimd.dma_start(out=h_parked(s).rearrange("(m w) -> m w", w=256), in_=zs[s][16 * NSEL : P, :])
+
+        def fetch_h(s, n):
+            base = (n - NSEL) * 16 * 256
+            nc.sync.dma_start(
+                out=hh[s][:].bitcast(F32)[:, 512 * (n - NSEL) : 512 * (n - NSEL) + 512],
+                in_=h_parked(s)[base : base + 16 * 256]
+                .rearrange("(c f) -> c f", f=512)
+                .unsqueeze(0)
+                .to_broadcast([16, 8, 512]),
             )
 
-        def permute_l(s, engine):
-            if engine == V:
-                for rep in range(2):
-                    nc.vector.tensor_copy(
-                        out=lq[s][:].bitcast(F32).rearrange("p (n a c g t) -> p n a c g t", a=16, c=2, g=2, t=2)[:, :, :, rep],
-                        in_=ld[s][:].bitcast(F32)[:, 64 * NCHIP : 512].rearrange("p (n t g a) -> p n a g t", t=2, g=2, a=16),
-                    )
-                return
-            for rep in range(2):
-                for g in range(2):
-                    copy_on(
-                        engine,
-                        lq[s][:].bitcast(F32).rearrange("p (n a c g t) -> p n a c g t", a=16, c=2, g=2, t=2)[:, :, :, rep, g, :],
-                        ld[s][:].bitcast(F32)[:, 64 * NCHIP : 512].rearrange("p (n t g a) -> p n a g t", t=2, g=2, a=16)[:, :, :, g, :],
-                    )
+        def prepare_l(s):
+            for g in range(2):
+                nc.vector.tensor_copy(
+                    out=ld[s][:].rearrange("p (n a g t e) -> p g n a t e", a=16, g=2, t=2, e=2)[:, g, :, 0 : 16 - g],
+                    in_=lr[s][:]
+                    .rearrange("p (n f) -> p n f", n=NB)[:, :, 0:62]
+                    .rearrange("p n (t a) -> p n a t", t=2)[:, :, 16 * g : 16 * g + 16 - g]
+                    .unsqueeze(4)
+                    .to_broadcast([P, NB, 16 - g, 2, 2]),
+                )
 
         def parked(s):
-            words = (NB - NCHIP) * P * P
+            words = (NB - NCHIP) * 64 * P
             base = NB * 65536 - (2 - s) * words
             return out.rearrange("n i j -> (n i j)")[base : base + words]
 
         def park_l(s, engine):
-            for lo in range(0, NB - NCHIP, 4):
-                hi = min(lo + 4, NB - NCHIP)
-                yps = ps_1.tile([P, 512], F32, name="acc")
-                for n in range(lo, hi):
-                    nc.tensor.transpose(
-                        yps[:, P * (n - lo) : P * (n - lo) + P], lq[s][:].bitcast(F32)[:, P * n : P * n + P], ident[:]
-                    )
-                copy_on(engine, ys[s][:, P * lo : P * hi], yps[:, 0 : P * (hi - lo)])
+            yps = ps_1.tile([P, 512], F32, name="acc")
+            pairs = (NB - NCHIP) // 2
+            for q in range(pairs):
+                o = P * (q + NCHIP // 2)
+                nc.tensor.transpose(yps[:, P * q : P * q + P], ld[s][:].bitcast(F32)[:, o : o + P], ident[:])
+            copy_on(engine, ys[s][:], yps[:, 0 : P * pairs])
             nc.gpsimd.dma_start(
-                out=parked(s).rearrange("(n m x) -> m n x", m=P, x=P),
-                in_=ys[s][:].rearrange("p (n x) -> p n x", x=P),
+                out=parked(s).rearrange("(q m x) -> m q x", m=P, x=P),
+                in_=ys[s][:].rearrange("p (q x) -> p q x", x=P),
             )
 
-        def fetch_l(s, n0, n1):
-            for o in range(4):
-                nc.sync.dma_start(
-                    out=ldd[s][:]
-                    .bitcast(F32)[o:P:4, 512 * (n0 - NCHIP) : 512 * (n1 - NCHIP)]
-                    .rearrange("p (n f) -> p n f", f=512),
-                    in_=parked(s).rearrange("(n i f) -> i n f", i=32, f=512)[:, n0 - NCHIP : n1 - NCHIP, :],
-                )
+        def fetch_l(s, n):
+            base = (n - NCHIP) * 64 * P
+            nc.sync.dma_start(
+                out=ldd[s][:].bitcast(F32)[:, 512 * (n - NCHIP) : 512 * (n - NCHIP) + 512],
+                in_=parked(s)[base : base + 64 * P]
+                .rearrange("(a f) -> a f", f=512)
+                .unsqueeze(1)
+                .to_broadcast([16, 8, 512]),
+            )
 
         def spread_l(n, s, engine):
             copy_on(
                 engine,
-                le[s][:].bitcast(F32)[:, 512 * n : 512 * n + 512].rearrange("p (k c) -> p k c", c=8),
-                ld[s][:].bitcast(F32)[:, 64 * n : 64 * n + 64].unsqueeze(2).to_broadcast([P, 64, 8]),
+                le[s][:].bitcast(F32)[:, 512 * n : 512 * n + 512].rearrange("p (q a c) -> p q a c", q=4, c=8),
+                ld[s][:]
+                .bitcast(F32)[:, 64 * n : 64 * n + 64]
+                .rearrange("p (a q) -> p q a", q=4)
+                .unsqueeze(3)
+                .to_broadcast([P, 4, 16, 8]),
             )
 
         def flip_l(n, s, engine):
             lps = ps_1.tile([P, 512], F32, name="acc")
-            for g in range(2):
-                for t in range(2):
-                    o = (2 * g + t) * P
-                    i = 512 * n + 256 * t + P * g
-                    nc.tensor.transpose(lps[:, o : o + P], le[s][:].bitcast(F32)[:, i : i + P], ident[:])
+            for q in range(4):
+                i = 512 * n + P * q
+                nc.tensor.transpose(lps[:, P * q : P * q + P], le[s][:].bitcast(F32)[:, i : i + P], ident[:])
             ls = work.tile([P, 1024], BF16, name="ls", bufs=2 * NCHIP)
             copy_on(engine, ls[:].bitcast(F32), lps[:])
             live["ls", n, s] = ls
@@ -186,7 +197,11 @@ def tile_qriaffine_kernel(tc, layer1, layer2, layer3, h1, h2, h3, W, out):
         def spread_h(n, s):
             nc.vector.tensor_copy(
                 out=hx[s][:].bitcast(F32)[:, 512 * n : 512 * n + 512].rearrange("p (t u a c) -> p t u a c", t=2, u=2, a=16),
-                in_=h_words(s)[:, 2 * n : 2 * n + 2]
+                in_=(
+                    hr[0][:].bitcast(F32).rearrange("p (k c u) -> p k u c", c=8, u=2)[:, 2 * n : 2 * n + 2]
+                    if s == 0
+                    else hq[1][:].bitcast(F32).rearrange("p (u n c t) -> p n t u c", u=2, c=8, t=2)[:, n]
+                )
                 .unsqueeze(3)
                 .to_broadcast([P, 2, 2, 16, 8]),
             )
@@ -230,9 +245,10 @@ def tile_qriaffine_kernel(tc, layer1, layer2, layer3, h1, h2, h3, W, out):
                             op=MULT,
                         )
                 return
+            hsrc = live["hps", n, s][:] if n < NSEL else hh[s][:, 1024 * (n - NSEL) : 1024 * (n - NSEL) + 1024]
             nc.vector.tensor_tensor(
                 out=grouped[:].rearrange("p (g w u e) -> p g w u e", g=2, u=2, e=2),
-                in0=live["hps", n, s][:]
+                in0=hsrc
                 .rearrange("p (w u e) -> p w u e", u=2, e=2)
                 .unsqueeze(1)
                 .to_broadcast([P, 2, 256, 2, 2]),
@@ -364,7 +380,8 @@ def tile_qriaffine_kernel(tc, layer1, layer2, layer3, h1, h2, h3, W, out):
         def prefetch(limit):
             while len(selected) < min(limit, len(order)):
                 n, s = order[len(selected)]
-                select_h(n, s)
+                if n < NSEL:
+                    select_h(n, s)
                 selected.append((n, s))
 
         load_x(0)
@@ -378,10 +395,10 @@ def tile_qriaffine_kernel(tc, layer1, layer2, layer3, h1, h2, h3, W, out):
         prefetch(1)
         prepare_l(0)
         spread_l(0, 0, V)
-        permute_l(0, V)
         flip_l(0, 0, A)
+        permute_h(0)
         flip_h(0, A)
-        permute_h()
+        permute_h(1)
         spread_h(0, 1)
         prefetch(2)
         prepare_l(1)
@@ -394,15 +411,17 @@ def tile_qriaffine_kernel(tc, layer1, layer2, layer3, h1, h2, h3, W, out):
         regroup_w(0, 1, A)
         spread_l(1, 0, V)
         multiply(0, 1)
-        permute_l(1, V)
         flip_l(1, 0, A)
         spread_l(1, 1, V)
         park_l(1, A)
         flip_l(1, 1, A)
         for s in range(2):
-            fetch_l(s, NCHIP, 4)
-        for s in range(2):
-            fetch_l(s, 4, NB)
+            park_h(s)
+        for n in range(NCHIP, NB):
+            for s in range(2):
+                fetch_l(s, n)
+                if n >= NSEL:
+                    fetch_h(s, n)
         quantise(0, 0)
         quantise(0, 1)
         prefetch(HBUFS + 2)

@@ -17,9 +17,9 @@ P = 128
 NB = 8
 V = "vector"
 A = "scalar"
-PINNED = True
 NCHIP = 2
-NHE = 1
+NPARK = 2
+NHE = 0
 NSEL = 4
 HBUFS = 4
 
@@ -31,8 +31,7 @@ def tile_qriaffine_kernel(tc, layer1, layer2, layer3, h1, h2, h3, W, out):
         work = ctx.enter_context(tc.tile_pool(name="work", bufs=3))
         ps_h = ctx.enter_context(tc.psum_pool(name="ps_h", bufs=HBUFS))
         ps_1 = ctx.enter_context(tc.psum_pool(name="ps_1", bufs=8 - HBUFS))
-        if PINNED:
-            ctx.enter_context(tc.manual_schedule())
+        ctx.enter_context(tc.manual_schedule())
 
         def copy_on(engine, dst, src):
             if engine == V:
@@ -50,7 +49,8 @@ def tile_qriaffine_kernel(tc, layer1, layer2, layer3, h1, h2, h3, W, out):
         hq = [keep.tile([P, 512], BF16, name="hq%d" % s) for s in range(2)]
         hh = [keep.tile([P, (NB - NSEL) * 1024], BF16, name="hh%d" % s) for s in range(2)]
         zs = [keep.tile([P, 256], F32, name="zs%d" % s) for s in range(2)]
-        ys = [keep.tile([P, (NB - NCHIP) * P // 2], F32, name="ys%d" % s) for s in range(2)]
+        lq = [keep.tile([P, (NB - NPARK) * P], BF16, name="lq%d" % s) for s in range(2)]
+        ys = [keep.tile([P, (NB - NPARK) * P // 2], F32, name="ys%d" % s) for s in range(2)]
         hx = [keep.tile([P, NHE * 1024], BF16, name="hx%d" % s) for s in range(2)]
         le = [keep.tile([P, NCHIP * 1024], BF16, name="le%d" % s) for s in range(2)]
         ldd = [keep.tile([P, (NB - NCHIP) * 1024], BF16, name="ldd%d" % s) for s in range(2)]
@@ -80,7 +80,7 @@ def tile_qriaffine_kernel(tc, layer1, layer2, layer3, h1, h2, h3, W, out):
         def constants():
             make_identity(nc, ident[:])
             for s in range(2):
-                nc.vector.memset(ld[s][:].rearrange("p (n a g f) -> p n a g f", a=16, g=2, f=4)[:, :, 15, 1, :], 1.0)
+                nc.vector.memset(ld[s][:].rearrange("p (q a e) -> p q a e", a=32, e=2)[:, :, 31, :], 1.0)
 
         def selectors():
             nc.vector.tensor_copy(out=identb[:], in_=ident[:])
@@ -120,7 +120,7 @@ def tile_qriaffine_kernel(tc, layer1, layer2, layer3, h1, h2, h3, W, out):
 
         def h_parked(s):
             words = (NB - NSEL) * 16 * 256
-            base = NB * 65536 - 2 * (NB - NCHIP) * 64 * P - (2 - s) * words
+            base = NB * 65536 - 2 * (NB - NPARK) * 64 * P - (2 - s) * words
             return out.rearrange("n i j -> (n i j)")[base : base + words]
 
         def park_h(s):
@@ -137,27 +137,33 @@ def tile_qriaffine_kernel(tc, layer1, layer2, layer3, h1, h2, h3, W, out):
             )
 
         def prepare_l(s):
-            for g in range(2):
-                nc.vector.tensor_copy(
-                    out=ld[s][:].rearrange("p (n a g t e) -> p g n a t e", a=16, g=2, t=2, e=2)[:, g, :, 0 : 16 - g],
-                    in_=lr[s][:]
-                    .rearrange("p (n f) -> p n f", n=NB)[:, :, 0:62]
-                    .rearrange("p n (t a) -> p n a t", t=2)[:, :, 16 * g : 16 * g + 16 - g]
-                    .unsqueeze(4)
-                    .to_broadcast([P, NB, 16 - g, 2, 2]),
-                )
+            nc.vector.tensor_copy(
+                out=ld[s][:].rearrange("p (n t a e) -> p n t a e", t=2, a=32, e=2)[:, :, :, 0:31, :],
+                in_=lr[s][:]
+                .rearrange("p (n f) -> p n f", n=NB)[:, :, 0:62]
+                .rearrange("p n (t a) -> p n t a", t=2)
+                .unsqueeze(4)
+                .to_broadcast([P, NB, 2, 31, 2]),
+            )
+
+        def permute_l(s):
+            nc.vector.tensor_copy(
+                out=lq[s][:].bitcast(F32).rearrange("p (n a g t) -> p n a g t", a=16, g=2, t=2),
+                in_=ld[s][:].bitcast(F32)[:, 64 * NPARK : 512].rearrange("p (n t g a) -> p n a g t", t=2, g=2, a=16),
+            )
 
         def parked(s):
-            words = (NB - NCHIP) * 64 * P
+            words = (NB - NPARK) * 64 * P
             base = NB * 65536 - (2 - s) * words
             return out.rearrange("n i j -> (n i j)")[base : base + words]
 
         def park_l(s, engine):
             yps = ps_1.tile([P, 512], F32, name="acc")
-            pairs = (NB - NCHIP) // 2
+            pairs = (NB - NPARK) // 2
             for q in range(pairs):
-                o = P * (q + NCHIP // 2)
-                nc.tensor.transpose(yps[:, P * q : P * q + P], ld[s][:].bitcast(F32)[:, o : o + P], ident[:])
+                nc.tensor.transpose(
+                    yps[:, P * q : P * q + P], lq[s][:].bitcast(F32)[:, P * q : P * q + P], ident[:]
+                )
             copy_on(engine, ys[s][:], yps[:, 0 : P * pairs])
             nc.gpsimd.dma_start(
                 out=parked(s).rearrange("(q m x) -> m q x", m=P, x=P),
@@ -165,7 +171,7 @@ def tile_qriaffine_kernel(tc, layer1, layer2, layer3, h1, h2, h3, W, out):
             )
 
         def fetch_l(s, n):
-            base = (n - NCHIP) * 64 * P
+            base = (n - NPARK) * 64 * P
             nc.sync.dma_start(
                 out=ldd[s][:].bitcast(F32)[:, 512 * (n - NCHIP) : 512 * (n - NCHIP) + 512],
                 in_=parked(s)[base : base + 64 * P]
@@ -177,19 +183,17 @@ def tile_qriaffine_kernel(tc, layer1, layer2, layer3, h1, h2, h3, W, out):
         def spread_l(n, s, engine):
             copy_on(
                 engine,
-                le[s][:].bitcast(F32)[:, 512 * n : 512 * n + 512].rearrange("p (q a c) -> p q a c", q=4, c=8),
-                ld[s][:]
-                .bitcast(F32)[:, 64 * n : 64 * n + 64]
-                .rearrange("p (a q) -> p q a", q=4)
-                .unsqueeze(3)
-                .to_broadcast([P, 4, 16, 8]),
+                le[s][:].bitcast(F32)[:, 512 * n : 512 * n + 512].rearrange("p (k c) -> p k c", c=8),
+                ld[s][:].bitcast(F32)[:, 64 * n : 64 * n + 64].unsqueeze(2).to_broadcast([P, 64, 8]),
             )
 
         def flip_l(n, s, engine):
             lps = ps_1.tile([P, 512], F32, name="acc")
-            for q in range(4):
-                i = 512 * n + P * q
-                nc.tensor.transpose(lps[:, P * q : P * q + P], le[s][:].bitcast(F32)[:, i : i + P], ident[:])
+            for g in range(2):
+                for t in range(2):
+                    o = (2 * g + t) * P
+                    i = 512 * n + 256 * t + P * g
+                    nc.tensor.transpose(lps[:, o : o + P], le[s][:].bitcast(F32)[:, i : i + P], ident[:])
             ls = work.tile([P, 1024], BF16, name="ls", bufs=2 * NCHIP)
             copy_on(engine, ls[:].bitcast(F32), lps[:])
             live["ls", n, s] = ls
@@ -233,17 +237,18 @@ def tile_qriaffine_kernel(tc, layer1, layer2, layer3, h1, h2, h3, W, out):
             live["grouped", n, s] = grouped
             if n < NHE:
                 for t in range(2):
-                    for g in range(2):
-                        nc.vector.tensor_tensor(
-                            out=grouped[:].rearrange("p (g t x u e) -> p g t x u e", t=2, g=2, u=2, e=2)[:, g, t],
-                            in0=live["hps", n, s][:]
-                            .bitcast(BF16)
-                            .rearrange("p (t u x e) -> p t x u e", t=2, u=2, e=2)[:, t],
-                            in1=lsrc.rearrange("p (g t x e) -> p g t x e", t=2, g=2, e=2)[:, g, t]
-                            .unsqueeze(2)
-                            .to_broadcast([P, P, 2, 2]),
-                            op=MULT,
-                        )
+                    nc.vector.tensor_tensor(
+                        out=grouped[:].rearrange("p (g t x u e) -> p g t x u e", t=2, g=2, u=2, e=2)[:, :, t],
+                        in0=live["hps", n, s][:]
+                        .bitcast(BF16)
+                        .rearrange("p (t u x e) -> p t x u e", t=2, u=2, e=2)[:, t]
+                        .unsqueeze(1)
+                        .to_broadcast([P, 2, P, 2, 2]),
+                        in1=lsrc.rearrange("p (g t x e) -> p g t x e", t=2, g=2, e=2)[:, :, t]
+                        .unsqueeze(3)
+                        .to_broadcast([P, 2, P, 2, 2]),
+                        op=MULT,
+                    )
                 return
             hsrc = live["hps", n, s][:] if n < NSEL else hh[s][:, 1024 * (n - NSEL) : 1024 * (n - NSEL) + 1024]
             nc.vector.tensor_tensor(
@@ -354,7 +359,7 @@ def tile_qriaffine_kernel(tc, layer1, layer2, layer3, h1, h2, h3, W, out):
             quantise_q(n, (t,))
             res = ps_1.tile([P, 512], F32, name="acc")
             second_passes(n, t, res[:, 0:256])
-            ob = work.tile([P, 512], F32, name="ob")
+            ob = work.tile([P, 512], F32, name="ob", bufs=6)
             copy_on(
                 engine,
                 ob[:, 0:256].rearrange("p (x s) -> p x s", s=2),
@@ -363,7 +368,7 @@ def tile_qriaffine_kernel(tc, layer1, layer2, layer3, h1, h2, h3, W, out):
             nc.sync.dma_start(out=out[n].rearrange("(x t) j -> x t j", t=2)[:, t, :], in_=ob[:, 0:256])
 
         def deliver(n, engine):
-            ob = work.tile([P, 512], F32, name="ob")
+            ob = work.tile([P, 512], F32, name="ob", bufs=6)
             copy_on(
                 engine,
                 ob[:].rearrange("p (t x s) -> p t x s", t=2, s=2),
@@ -391,30 +396,32 @@ def tile_qriaffine_kernel(tc, layer1, layer2, layer3, h1, h2, h3, W, out):
                 load_w(g, c8)
         constants()
         selectors()
-        spread_h(0, 0)
-        prefetch(1)
-        prepare_l(0)
-        spread_l(0, 0, V)
-        flip_l(0, 0, A)
         permute_h(0)
         flip_h(0, A)
+        prepare_l(0)
+        spread_l(1, 0, A)
+        spread_l(0, 0, V)
+        flip_l(0, 0, A)
+        prefetch(1)
         permute_h(1)
-        spread_h(0, 1)
-        prefetch(2)
-        prepare_l(1)
-        spread_l(0, 1, V)
-        park_l(0, A)
-        flip_l(0, 1, A)
-        multiply(0, 0)
         flip_h(1, A)
-        prefetch(4)
-        regroup_w(0, 1, A)
-        spread_l(1, 0, V)
-        multiply(0, 1)
+        prepare_l(1)
+        spread_l(1, 1, A)
+        spread_l(0, 1, V)
+        flip_l(0, 1, A)
+        prefetch(2)
+        permute_l(0)
+        permute_l(1)
         flip_l(1, 0, A)
-        spread_l(1, 1, V)
-        park_l(1, A)
+        prefetch(3)
         flip_l(1, 1, A)
+        prefetch(4)
+        multiply(0, 0)
+        park_l(0, A)
+        park_l(1, A)
+        quantise(0, 0)
+        multiply(0, 1)
+        regroup_w(0, 1, A)
         for s in range(2):
             park_h(s)
         for n in range(NCHIP, NB):
@@ -422,48 +429,46 @@ def tile_qriaffine_kernel(tc, layer1, layer2, layer3, h1, h2, h3, W, out):
                 fetch_l(s, n)
                 if n >= NSEL:
                     fetch_h(s, n)
-        quantise(0, 0)
-        quantise(0, 1)
-        prefetch(HBUFS + 2)
+        multiply(1, 0)
         regroup_w(0, 0, V)
         keep_warm(0, 0, 1)
+        prefetch(HBUFS + 2)
+        quantise(0, 1)
+        quantise_w(0, 0)
+        multiply(1, 1)
+        quantise(1, 0)
+        prefetch(HBUFS + 4)
         regroup_w(1, 1, A)
         regroup_w(1, 0, V)
         keep_warm(1, 0, 2)
-        quantise_w(0, 0)
+        quantise_w(0, 1)
         quantise_w(1, 0)
         for b in (0, 2):
             first_product(0, b)
             fetch_q(0, b, A)
-        multiply(1, 0)
-        prefetch(HBUFS + 3)
-        quantise_w(0, 1)
+        quantise(1, 1)
         quantise_w(1, 1)
         for b in (1, 3):
             first_product(0, b)
             fetch_q(0, b, A)
-        quantise(1, 0)
-        multiply(1, 1)
-        prefetch(HBUFS + 4)
         for r in range(2, NB + 2):
             if r < NB:
                 multiply(r, 0)
-            if r >= 3:
+            if r >= 4:
                 quantise(r - 2, 1)
-            if r - 2 < NB - 1:
-                quantise_q(r - 2)
             if r < NB:
                 quantise(r, 0)
             if 3 <= r <= NB:
                 multiply(r - 1, 1)
+            if r - 2 < NB - 1:
+                quantise_q(r - 2)
             if r <= NB:
                 for b in range(4):
                     first_product(r - 1, b)
                     fetch_q(r - 1, b, A)
-            if r - 2 < NB - 1:
-                second_product(r - 2)
-                deliver(r - 2, A)
-            else:
-                finish_half(r - 2, 0, A)
-                finish_half(r - 2, 1, V)
-            prefetch(HBUFS + 2 * r + (1 if r >= 3 else 1))
+            if r >= 3:
+                second_product(r - 3)
+                deliver(r - 3, A)
+            prefetch(HBUFS + 2 * r + 1)
+        finish_half(NB - 1, 0, A)
+        finish_half(NB - 1, 1, V)

@@ -124,7 +124,7 @@ def tile_qriaffine_kernel(tc, layer1, layer2, layer3, h1, h2, h3, W, out):
             return out.rearrange("n i j -> (n i j)")[base : base + words]
 
         def park_h(s):
-            nc.gpsimd.dma_start(out=h_parked(s).rearrange("(m w) -> m w", w=256), in_=zs[s][16 * NSEL : P, :])
+            nc.sync.dma_start(out=h_parked(s).rearrange("(m w) -> m w", w=256), in_=zs[s][16 * NSEL : P, :])
 
         def fetch_h(s, n):
             base = (n - NSEL) * 16 * 256
@@ -165,7 +165,9 @@ def tile_qriaffine_kernel(tc, layer1, layer2, layer3, h1, h2, h3, W, out):
                     yps[:, P * q : P * q + P], lq[s][:].bitcast(F32)[:, P * q : P * q + P], ident[:]
                 )
             copy_on(engine, ys[s][:], yps[:, 0 : P * pairs])
-            nc.gpsimd.dma_start(
+
+        def store_l(s):
+            nc.sync.dma_start(
                 out=parked(s).rearrange("(q m x) -> m q x", m=P, x=P),
                 in_=ys[s][:].rearrange("p (q x) -> p q x", x=P),
             )
@@ -391,9 +393,10 @@ def tile_qriaffine_kernel(tc, layer1, layer2, layer3, h1, h2, h3, W, out):
 
         load_x(0)
         load_x(1)
-        for g in range(2):
-            for c8 in (0, 4, 1, 5, 2, 6, 3, 7):
-                load_w(g, c8)
+        for c8 in (0, 4, 1, 5, 2, 6, 3, 7):
+            load_w(0, c8)
+        for c8 in (0, 4, 1, 5, 2, 6, 3, 7):
+            load_w(1, c8)
         constants()
         selectors()
         permute_h(0)
@@ -419,12 +422,15 @@ def tile_qriaffine_kernel(tc, layer1, layer2, layer3, h1, h2, h3, W, out):
         multiply(0, 0)
         park_l(0, A)
         park_l(1, A)
+        for s in range(2):
+            store_l(s)
         quantise(0, 0)
         multiply(0, 1)
         regroup_w(0, 1, A)
-        for s in range(2):
-            park_h(s)
         for n in range(NCHIP, NB):
+            if n == NSEL:
+                for s in range(2):
+                    park_h(s)
             for s in range(2):
                 fetch_l(s, n)
                 if n >= NSEL:

@@ -17,7 +17,7 @@ P = 128
 NB = 8
 V = "vector"
 A = "scalar"
-NCHIP = 2
+NCHIP = 3
 NPARK = 2
 NHE = 0
 NSEL = 4
@@ -378,17 +378,13 @@ def tile_qriaffine_kernel(tc, layer1, layer2, layer3, h1, h2, h3, W, out):
             )
             nc.sync.dma_start(out=out[n].rearrange("(x t) j -> x (t j)", t=2), in_=ob[:])
 
-        order = [(0, 0), (0, 1), (1, 0), (1, 1), (2, 0)]
-        for n in range(3, NB):
-            order.extend([(n, 0), (n - 1, 1)])
-        order.append((NB - 1, 1))
+        order = [(n, s) for n in range(NSEL) for s in range(2)]
         selected = []
 
         def prefetch(limit):
             while len(selected) < min(limit, len(order)):
                 n, s = order[len(selected)]
-                if n < NSEL:
-                    select_h(n, s)
+                select_h(n, s)
                 selected.append((n, s))
 
         load_x(0)
@@ -426,6 +422,8 @@ def tile_qriaffine_kernel(tc, layer1, layer2, layer3, h1, h2, h3, W, out):
             store_l(s)
         quantise(0, 0)
         multiply(0, 1)
+        spread_l(2, 0, A)
+        flip_l(2, 0, A)
         regroup_w(0, 1, A)
         for n in range(NCHIP, NB):
             if n == NSEL:
@@ -443,8 +441,10 @@ def tile_qriaffine_kernel(tc, layer1, layer2, layer3, h1, h2, h3, W, out):
         quantise_w(0, 0)
         multiply(1, 1)
         quantise(1, 0)
+        multiply(2, 0)
         prefetch(HBUFS + 4)
         regroup_w(1, 1, A)
+        spread_l(2, 1, A)
         regroup_w(1, 0, V)
         keep_warm(1, 0, 2)
         quantise_w(0, 1)
@@ -453,28 +453,32 @@ def tile_qriaffine_kernel(tc, layer1, layer2, layer3, h1, h2, h3, W, out):
             first_product(0, b)
             fetch_q(0, b, A)
         quantise(1, 1)
+        flip_l(2, 1, A)
         quantise_w(1, 1)
         for b in (1, 3):
             first_product(0, b)
             fetch_q(0, b, A)
-        for r in range(2, NB + 2):
+        due = {3: (0,), 4: (1,), 5: (2,), 6: (3,), 7: (4, 5), 8: (6,)}
+        quantise(2, 0)
+        for b in range(4):
+            first_product(1, b)
+            fetch_q(1, b, A)
+        for r in range(3, NB + 2):
             if r < NB:
                 multiply(r, 0)
             if r >= 4:
                 quantise(r - 2, 1)
             if r < NB:
                 quantise(r, 0)
-            if 3 <= r <= NB:
-                multiply(r - 1, 1)
-            if r - 2 < NB - 1:
-                quantise_q(r - 2)
             if r <= NB:
+                multiply(r - 1, 1)
                 for b in range(4):
                     first_product(r - 1, b)
                     fetch_q(r - 1, b, A)
-            if r >= 3:
-                second_product(r - 3)
-                deliver(r - 3, A)
-            prefetch(HBUFS + 2 * r + 1)
+            for n in due.get(r, ()):
+                quantise_q(n)
+            for n in due.get(r, ()):
+                second_product(n)
+                deliver(n, A)
         finish_half(NB - 1, 0, A)
         finish_half(NB - 1, 1, V)

@@ -424,7 +424,7 @@ def tile_qriaffine_kernel(tc, layer1, layer2, layer3, h1, h2, h3, W, out):
         multiply(0, 1)
         spread_l(2, 0, A)
         flip_l(2, 0, A)
-        regroup_w(0, 1, A)
+        spread_l(2, 1, A)
         for n in range(NCHIP, NB):
             if n == NSEL:
                 for s in range(2):
@@ -434,17 +434,20 @@ def tile_qriaffine_kernel(tc, layer1, layer2, layer3, h1, h2, h3, W, out):
                 if n >= NSEL:
                     fetch_h(s, n)
         multiply(1, 0)
-        regroup_w(0, 0, V)
-        keep_warm(0, 0, 1)
         prefetch(HBUFS + 2)
+        flip_l(2, 1, A)
+        regroup_w(0, 1, A)
         quantise(0, 1)
-        quantise_w(0, 0)
         multiply(1, 1)
         quantise(1, 0)
-        multiply(2, 0)
+        regroup_w(0, 0, V)
+        keep_warm(0, 0, 1)
         prefetch(HBUFS + 4)
+        multiply(2, 0)
+        quantise_w(0, 0)
+        quantise(1, 1)
+        multiply(2, 1)
         regroup_w(1, 1, A)
-        spread_l(2, 1, A)
         regroup_w(1, 0, V)
         keep_warm(1, 0, 2)
         quantise_w(0, 1)
@@ -452,26 +455,27 @@ def tile_qriaffine_kernel(tc, layer1, layer2, layer3, h1, h2, h3, W, out):
         for b in (0, 2):
             first_product(0, b)
             fetch_q(0, b, A)
-        quantise(1, 1)
-        flip_l(2, 1, A)
+        quantise(2, 0)
         quantise_w(1, 1)
         for b in (1, 3):
             first_product(0, b)
             fetch_q(0, b, A)
-        due = {3: (0,), 4: (1,), 5: (2,), 6: (3,), 7: (4, 5), 8: (6,)}
-        quantise(2, 0)
+        due = {3: (), 4: (0,), 5: (1, 2), 6: (3,), 7: (4, 5), 8: (6,)}
         for b in range(4):
             first_product(1, b)
             fetch_q(1, b, A)
         for r in range(3, NB + 2):
             if r < NB:
                 multiply(r, 0)
-            if r >= 4:
+            if r == 3:
+                quantise(2, 1)
+            elif r >= 5:
                 quantise(r - 2, 1)
             if r < NB:
                 quantise(r, 0)
-            if r <= NB:
+            if 4 <= r <= NB:
                 multiply(r - 1, 1)
+            if r <= NB:
                 for b in range(4):
                     first_product(r - 1, b)
                     fetch_q(r - 1, b, A)

@@ -19,9 +19,10 @@ V = "vector"
 A = "scalar"
 NCHIP = 3
 NPARK = 2
-NHE = 0
 NSEL = 4
 HBUFS = 4
+SLOTS = 2 * NB + 2
+PAIRS = (4, 5, 6)
 
 
 def tile_qriaffine_kernel(tc, layer1, layer2, layer3, h1, h2, h3, W, out):
@@ -41,41 +42,48 @@ def tile_qriaffine_kernel(tc, layer1, layer2, layer3, h1, h2, h3, W, out):
 
         lr = [keep.tile([P, 512], BF16, name="lr%d" % s) for s in range(2)]
         hr = [keep.tile([P, 512], BF16, name="hr%d" % s) for s in range(2)]
-        wr = [keep.tile([P, 4096], BF16, name="wr%d" % g) for g in range(2)]
+        wr = keep.tile([P, 8192], BF16, name="wr")
         ident = keep.tile([P, P], F32, name="ident")
         identb = keep.tile([P, P], BF16, name="identb")
         selh = keep.tile([P, 2 * NSEL * P], BF16, name="selh")
         ld = [keep.tile([P, 1024], BF16, name="ld%d" % s) for s in range(2)]
         hq = [keep.tile([P, 512], BF16, name="hq%d" % s) for s in range(2)]
-        hh = [keep.tile([P, (NB - NSEL) * 1024], BF16, name="hh%d" % s) for s in range(2)]
+        hh = keep.tile([P, (SLOTS - 2 * NSEL) * 1024], BF16, name="hh")
         zs = [keep.tile([P, 256], F32, name="zs%d" % s) for s in range(2)]
-        lq = [keep.tile([P, (NB - NPARK) * P], BF16, name="lq%d" % s) for s in range(2)]
+        lq = [keep.tile([P, NB * P], BF16, name="lq%d" % s) for s in range(2)]
         ys = [keep.tile([P, (NB - NPARK) * P // 2], F32, name="ys%d" % s) for s in range(2)]
-        hx = [keep.tile([P, NHE * 1024], BF16, name="hx%d" % s) for s in range(2)]
         le = [keep.tile([P, NCHIP * 1024], BF16, name="le%d" % s) for s in range(2)]
-        ldd = [keep.tile([P, (NB - NCHIP) * 1024], BF16, name="ldd%d" % s) for s in range(2)]
-        codes = [keep.tile([P, 4096], U32, name="codes%d" % s, align_bytes=64) for s in range(2)]
-        planes = [keep.tile([P, 4096], U8, name="planes%d" % s, align_bytes=64) for s in range(2)]
+        ldd = keep.tile([P, (SLOTS - 2 * NCHIP) * 1024], BF16, name="ldd")
+        codes = keep.tile([P, SLOTS * 512], U32, name="codes", align_bytes=64)
+        planes = keep.tile([P, SLOTS * 512], U8, name="planes", align_bytes=64)
         wg = keep.tile([P, 8192], BF16, name="wg", align_bytes=64)
         wc = keep.tile([P, 2048], U32, name="wc", align_bytes=64)
         ws = keep.tile([P, 2048], U8, name="ws", align_bytes=64)
         live = {}
 
-        def load_x(s):
-            nc.sync.dma_start(
+        def slot(n, s):
+            return 2 * n + 3 * s
+
+        def load_h(s):
+            nc.scalar.dma_start(
                 out=hr[s][:].rearrange("p (n f) -> p n f", n=NB),
                 in_=(h1, h2)[s].rearrange("n (x t) a -> x n (t a)", t=2),
             )
+
+        def load_l(s):
             nc.sync.dma_start(
                 out=lr[s][:].rearrange("p (n f) -> p n f", n=NB)[:, :, 0:62],
                 in_=(layer1, layer2)[s].rearrange("n (x t) a -> x n (t a)", t=2),
             )
 
-        def load_w(g, c8):
+        def load_w(c8):
             nc.sync.dma_start(
-                out=wr[g][c8:P:8, :].rearrange("p (b f) -> p b f", b=32),
-                in_=W[16 * g : 16 * g + 16, :, 4 * c8 : 4 * c8 + 4, :].rearrange("a b j d -> a b (j d)"),
+                out=wr[c8:P:8, :].rearrange("p (b f) -> p b f", f=128),
+                in_=W[:, :, 4 * c8 : 4 * c8 + 4, :].rearrange("(i g) b j d -> i (g b) (j d)", g=2),
             )
+
+        def w_rows(g, g2):
+            return wr[:, 4096 * g : 4096 * g + 4096].rearrange("p (m h j t d) -> p h t m d j", m=16, h=2, j=4, t=4, d=8)[:, g2]
 
         def constants():
             make_identity(nc, ident[:])
@@ -129,7 +137,7 @@ def tile_qriaffine_kernel(tc, layer1, layer2, layer3, h1, h2, h3, W, out):
         def fetch_h(s, n):
             base = (n - NSEL) * 16 * 256
             nc.sync.dma_start(
-                out=hh[s][:].bitcast(F32)[:, 512 * (n - NSEL) : 512 * (n - NSEL) + 512],
+                out=hh[:].bitcast(F32)[:, 512 * (slot(n, s) - 2 * NSEL) : 512 * (slot(n, s) - 2 * NSEL) + 512],
                 in_=h_parked(s)[base : base + 16 * 256]
                 .rearrange("(c f) -> c f", f=512)
                 .unsqueeze(0)
@@ -148,8 +156,8 @@ def tile_qriaffine_kernel(tc, layer1, layer2, layer3, h1, h2, h3, W, out):
 
         def permute_l(s):
             nc.vector.tensor_copy(
-                out=lq[s][:].bitcast(F32).rearrange("p (n a g t) -> p n a g t", a=16, g=2, t=2),
-                in_=ld[s][:].bitcast(F32)[:, 64 * NPARK : 512].rearrange("p (n t g a) -> p n a g t", t=2, g=2, a=16),
+                out=lq[s][:].bitcast(F32).rearrange("p (n i g t) -> p n i g t", i=16, g=2, t=2),
+                in_=ld[s][:].bitcast(F32).rearrange("p (n t i g) -> p n i g t", t=2, g=2, i=16),
             )
 
         def parked(s):
@@ -161,9 +169,8 @@ def tile_qriaffine_kernel(tc, layer1, layer2, layer3, h1, h2, h3, W, out):
             yps = ps_1.tile([P, 512], F32, name="acc")
             pairs = (NB - NPARK) // 2
             for q in range(pairs):
-                nc.tensor.transpose(
-                    yps[:, P * q : P * q + P], lq[s][:].bitcast(F32)[:, P * q : P * q + P], ident[:]
-                )
+                o = P * (q + NPARK // 2)
+                nc.tensor.transpose(yps[:, P * q : P * q + P], lq[s][:].bitcast(F32)[:, o : o + P], ident[:])
             copy_on(engine, ys[s][:], yps[:, 0 : P * pairs])
 
         def store_l(s):
@@ -175,7 +182,7 @@ def tile_qriaffine_kernel(tc, layer1, layer2, layer3, h1, h2, h3, W, out):
         def fetch_l(s, n):
             base = (n - NPARK) * 64 * P
             nc.sync.dma_start(
-                out=ldd[s][:].bitcast(F32)[:, 512 * (n - NCHIP) : 512 * (n - NCHIP) + 512],
+                out=ldd[:].bitcast(F32)[:, 512 * (slot(n, s) - 2 * NCHIP) : 512 * (slot(n, s) - 2 * NCHIP) + 512],
                 in_=parked(s)[base : base + 64 * P]
                 .rearrange("(a f) -> a f", f=512)
                 .unsqueeze(1)
@@ -185,42 +192,32 @@ def tile_qriaffine_kernel(tc, layer1, layer2, layer3, h1, h2, h3, W, out):
         def spread_l(n, s, engine):
             copy_on(
                 engine,
-                le[s][:].bitcast(F32)[:, 512 * n : 512 * n + 512].rearrange("p (k c) -> p k c", c=8),
-                ld[s][:].bitcast(F32)[:, 64 * n : 64 * n + 64].unsqueeze(2).to_broadcast([P, 64, 8]),
+                le[s][:].bitcast(F32)[:, 512 * n : 512 * n + 512].rearrange("p (g t i c) -> p g t i c", g=2, t=2, c=8)
+                if engine == V
+                else le[s][:].bitcast(F32)[:, 512 * n : 512 * n + 512].rearrange("p (q i c) -> p q i c", q=4, c=8),
+                ld[s][:]
+                .bitcast(F32)[:, 64 * n : 64 * n + 64]
+                .rearrange("p (t i g) -> p g t i", t=2, g=2)
+                .unsqueeze(4)
+                .to_broadcast([P, 2, 2, 16, 8])
+                if engine == V
+                else lq[s][:]
+                .bitcast(F32)[:, 64 * n : 64 * n + 64]
+                .rearrange("p (i q) -> p q i", q=4)
+                .unsqueeze(3)
+                .to_broadcast([P, 4, 16, 8]),
             )
 
         def flip_l(n, s, engine):
             lps = ps_1.tile([P, 512], F32, name="acc")
-            for g in range(2):
-                for t in range(2):
-                    o = (2 * g + t) * P
-                    i = 512 * n + 256 * t + P * g
-                    nc.tensor.transpose(lps[:, o : o + P], le[s][:].bitcast(F32)[:, i : i + P], ident[:])
+            for q in range(4):
+                i = 512 * n + P * q
+                nc.tensor.transpose(lps[:, P * q : P * q + P], le[s][:].bitcast(F32)[:, i : i + P], ident[:])
             ls = work.tile([P, 1024], BF16, name="ls", bufs=2 * NCHIP)
             copy_on(engine, ls[:].bitcast(F32), lps[:])
             live["ls", n, s] = ls
 
-        def spread_h(n, s):
-            nc.vector.tensor_copy(
-                out=hx[s][:].bitcast(F32)[:, 512 * n : 512 * n + 512].rearrange("p (t u a c) -> p t u a c", t=2, u=2, a=16),
-                in_=(
-                    hr[0][:].bitcast(F32).rearrange("p (k c u) -> p k u c", c=8, u=2)[:, 2 * n : 2 * n + 2]
-                    if s == 0
-                    else hq[1][:].bitcast(F32).rearrange("p (u n c t) -> p n t u c", u=2, c=8, t=2)[:, n]
-                )
-                .unsqueeze(3)
-                .to_broadcast([P, 2, 2, 16, 8]),
-            )
-
         def select_h(n, s):
-            if n < NHE:
-                hpf = ps_h.tile([P, 512], F32, name="hps")
-                for o in range(0, 512, P):
-                    nc.tensor.transpose(
-                        hpf[:, o : o + P], hx[s][:].bitcast(F32)[:, 512 * n + o : 512 * n + o + P], ident[:]
-                    )
-                live["hps", n, s] = hpf
-                return
             hps = ps_h.tile([P, 1024], BF16, name="hps")
             for t in range(2):
                 k = 2 * n + t
@@ -233,54 +230,99 @@ def tile_qriaffine_kernel(tc, layer1, layer2, layer3, h1, h2, h3, W, out):
                 )
             live["hps", n, s] = hps
 
+        def room(n, s):
+            if n + s not in PAIRS:
+                if ("grouped", n, s) not in live:
+                    grouped = work.tile([P, 2048], BF16, name="grouped", align_bytes=64)
+                    live["grouped", n, s] = grouped
+                return live["grouped", n, s][:]
+            if ("pair", n + s) not in live:
+                pair = work.tile([P, 4096], BF16, name="pair", align_bytes=64, bufs=2)
+                live["pair", n + s] = pair
+            return live["pair", n + s][:, 2048 * s : 2048 * s + 2048]
+
+        def l_source(n, s):
+            if n < NCHIP:
+                return live["ls", n, s][:]
+            o = 1024 * (slot(n, s) - 2 * NCHIP)
+            return ldd[:, o : o + 1024]
+
+        def h_source(n, s):
+            if n < NSEL:
+                return live["hps", n, s][:]
+            o = 1024 * (slot(n, s) - 2 * NSEL)
+            return hh[:, o : o + 1024]
+
         def multiply(n, s):
-            grouped = work.tile([P, 2048], BF16, name="grouped", align_bytes=64)
-            lsrc = live["ls", n, s][:] if n < NCHIP else ldd[s][:, 1024 * (n - NCHIP) : 1024 * (n - NCHIP) + 1024]
-            live["grouped", n, s] = grouped
-            if n < NHE:
-                for t in range(2):
-                    nc.vector.tensor_tensor(
-                        out=grouped[:].rearrange("p (g t x u e) -> p g t x u e", t=2, g=2, u=2, e=2)[:, :, t],
-                        in0=live["hps", n, s][:]
-                        .bitcast(BF16)
-                        .rearrange("p (t u x e) -> p t x u e", t=2, u=2, e=2)[:, t]
-                        .unsqueeze(1)
-                        .to_broadcast([P, 2, P, 2, 2]),
-                        in1=lsrc.rearrange("p (g t x e) -> p g t x e", t=2, g=2, e=2)[:, :, t]
-                        .unsqueeze(3)
-                        .to_broadcast([P, 2, P, 2, 2]),
-                        op=MULT,
-                    )
-                return
-            hsrc = live["hps", n, s][:] if n < NSEL else hh[s][:, 1024 * (n - NSEL) : 1024 * (n - NSEL) + 1024]
             nc.vector.tensor_tensor(
-                out=grouped[:].rearrange("p (g w u e) -> p g w u e", g=2, u=2, e=2),
-                in0=hsrc
+                out=room(n, s).rearrange("p (g w u e) -> p g w u e", g=2, u=2, e=2),
+                in0=h_source(n, s)
                 .rearrange("p (w u e) -> p w u e", u=2, e=2)
                 .unsqueeze(1)
                 .to_broadcast([P, 2, 256, 2, 2]),
-                in1=lsrc.rearrange("p (g w e) -> p g w e", g=2, e=2).unsqueeze(3).to_broadcast([P, 2, 256, 2, 2]),
+                in1=l_source(n, s)
+                .rearrange("p (g w e) -> p g w e", g=2, e=2)
+                .unsqueeze(3)
+                .to_broadcast([P, 2, 256, 2, 2]),
                 op=MULT,
             )
-            live["grouped", n, s] = grouped
+
+        def multiply_pair(m):
+            if m - 1 < NSEL:
+                multiply(m, 0)
+                multiply(m - 1, 1)
+                return
+            room(m, 0)
+            ho = 1024 * (slot(m, 0) - 2 * NSEL)
+            lo = 1024 * (slot(m, 0) - 2 * NCHIP)
+            nc.vector.tensor_tensor(
+                out=live["pair", m][:].rearrange("p (s g f) -> p s g f", s=2, g=2),
+                in0=hh[:, ho : ho + 2048]
+                .rearrange("p (s f) -> p s f", s=2)
+                .unsqueeze(2)
+                .to_broadcast([P, 2, 2, 1024]),
+                in1=ldd[:, lo : lo + 2048]
+                .rearrange("p (w e) -> p w e", e=2)
+                .unsqueeze(2)
+                .to_broadcast([P, 1024, 2, 2]),
+                op=MULT,
+            )
+
+        def quantise_slots(first, count, source):
+            o = 512 * first
+            w = 512 * count
+            nc.vector.quantize_mx(
+                out=codes[:, o : o + w].bitcast(FP8X4),
+                scales=planes[:, o : o + w],
+                in_=source,
+            )
 
         def quantise(n, s):
-            nc.vector.quantize_mx(
-                out=codes[s][:, 512 * n : 512 * n + 512].bitcast(FP8X4),
-                scales=planes[s][:, 512 * n : 512 * n + 512],
-                in_=live["grouped", n, s][:],
-            )
+            quantise_slots(slot(n, s), 1, room(n, s))
+
+        def quantise_pair(m):
+            quantise_slots(slot(m, 0), 2, live["pair", m][:])
 
         def regroup_w(g, g2, engine, t0=0, t1=4):
             dst = wg[:, 4096 * g + 2048 * g2 : 4096 * g + 2048 * g2 + 2048].rearrange(
                 "p (t b d j) -> p t b d j", t=4, b=16, d=8, j=4
             )
-            src = wr[g][:, 2048 * g2 : 2048 * g2 + 2048].rearrange("p (b j t d) -> p t b d j", b=16, j=4, t=4, d=8)
+            src = w_rows(g, g2)
             if engine == V:
                 nc.vector.tensor_copy(out=dst[:, t0:t1], in_=src[:, t0:t1])
             else:
                 for t in range(t0, t1):
                     nc.scalar.copy(out=dst[:, t], in_=src[:, t])
+
+        def interleave_w(g, g2, h, engine):
+            src = w_rows(g, g2)
+            wps = ps_1.tile([P, 1024], BF16, name="acc")
+            for i in range(2):
+                nc.tensor.matmul(
+                    out=wps[:, 512 * i : 512 * i + 512], lhsT=identb[:], rhs=src[:, 2 * h + i], start=True, stop=True
+                )
+            o = 4096 * g + 2048 * g2 + 1024 * h
+            copy_on(engine, wg[:, o : o + 1024], wps[:])
 
         def keep_warm(g, g2, times):
             for i in range(times):
@@ -302,13 +344,13 @@ def tile_qriaffine_kernel(tc, layer1, layer2, layer3, h1, h2, h3, W, out):
             for tt in range(4):
                 for g in range(2):
                     wo = 1024 * g + 512 * g2 + P * tt
-                    po = 512 * n + 256 * g + P * t
+                    po = 512 * slot(n, 0) + 256 * g + P * t
                     nc.tensor.matmul_mx(
                         out=acc[:, P * tt : P * tt + P],
                         lhsT=wc[:, wo : wo + P].bitcast(FP8X4),
                         lhsT_scale=ws[:, wo : wo + P],
-                        rhs=codes[0][:, po : po + P].bitcast(FP8X4),
-                        rhs_scale=planes[0][:, po : po + P],
+                        rhs=codes[:, po : po + P].bitcast(FP8X4),
+                        rhs_scale=planes[:, po : po + P],
                         start=(g == 0),
                         stop=(g == 1),
                     )
@@ -340,13 +382,13 @@ def tile_qriaffine_kernel(tc, layer1, layer2, layer3, h1, h2, h3, W, out):
         def second_passes(n, t, dst):
             for g2 in range(2):
                 qo = 256 * t + P * g2
-                ro = 512 * n + 256 * g2
+                ro = 512 * slot(n, 1) + 256 * g2
                 nc.tensor.matmul_mx(
                     out=dst,
                     lhsT=live["qc", n][:, qo : qo + P].bitcast(FP8X4),
                     lhsT_scale=live["qs", n][:, qo : qo + P],
-                    rhs=codes[1][:, ro : ro + 256].bitcast(FP8X4),
-                    rhs_scale=planes[1][:, ro : ro + 256],
+                    rhs=codes[:, ro : ro + 256].bitcast(FP8X4),
+                    rhs_scale=planes[:, ro : ro + 256],
                     start=(g2 == 0),
                     stop=(g2 == 1),
                 )
@@ -357,26 +399,27 @@ def tile_qriaffine_kernel(tc, layer1, layer2, layer3, h1, h2, h3, W, out):
                 second_passes(n, t, res[:, 256 * t : 256 * t + 256])
             live["res", n] = res
 
-        def finish_half(n, t, engine):
-            quantise_q(n, (t,))
-            res = ps_1.tile([P, 512], F32, name="acc")
-            second_passes(n, t, res[:, 0:256])
-            ob = work.tile([P, 512], F32, name="ob", bufs=6)
-            copy_on(
-                engine,
-                ob[:, 0:256].rearrange("p (x s) -> p x s", s=2),
-                res[:, 0:256].rearrange("p (s x) -> p x s", s=2),
-            )
-            nc.sync.dma_start(out=out[n].rearrange("(x t) j -> x t j", t=2)[:, t, :], in_=ob[:, 0:256])
+        def finish(n):
+            for t in range(2):
+                quantise_q(n, (t,))
+            for t in range(2):
+                res = ps_1.tile([P, 512], F32, name="acc")
+                second_passes(n, t, res[:, 0:256])
+                ob = work.tile([P, 512], F32, name="ob", bufs=6)
+                nc.vector.tensor_copy(
+                    out=ob[:, 0:256].rearrange("p (x s) -> p x s", s=2),
+                    in_=res[:, 0:256].rearrange("p (s x) -> p x s", s=2),
+                )
+                nc.sync.dma_start(out=out[n].rearrange("(x t) j -> x t j", t=2)[:, t, :], in_=ob[:, 0:256])
 
-        def deliver(n, engine):
+        def deliver(n, engine, queue):
             ob = work.tile([P, 512], F32, name="ob", bufs=6)
             copy_on(
                 engine,
                 ob[:].rearrange("p (t x s) -> p t x s", t=2, s=2),
                 live["res", n][:].rearrange("p (t s x) -> p t x s", t=2, s=2),
             )
-            nc.sync.dma_start(out=out[n].rearrange("(x t) j -> x (t j)", t=2), in_=ob[:])
+            queue.dma_start(out=out[n].rearrange("(x t) j -> x (t j)", t=2), in_=ob[:])
 
         order = [(n, s) for n in range(NSEL) for s in range(2)]
         selected = []
@@ -387,44 +430,43 @@ def tile_qriaffine_kernel(tc, layer1, layer2, layer3, h1, h2, h3, W, out):
                 select_h(n, s)
                 selected.append((n, s))
 
-        load_x(0)
-        load_x(1)
+        for s in range(2):
+            load_l(s)
+            load_h(s)
         for c8 in (0, 4, 1, 5, 2, 6, 3, 7):
-            load_w(0, c8)
-        for c8 in (0, 4, 1, 5, 2, 6, 3, 7):
-            load_w(1, c8)
+            load_w(c8)
         constants()
         selectors()
+        prepare_l(0)
         permute_h(0)
         flip_h(0, A)
-        prepare_l(0)
-        spread_l(1, 0, A)
         spread_l(0, 0, V)
+        permute_l(0)
         flip_l(0, 0, A)
         prefetch(1)
+        spread_l(1, 0, A)
+        prepare_l(1)
         permute_h(1)
         flip_h(1, A)
-        prepare_l(1)
-        spread_l(1, 1, A)
         spread_l(0, 1, V)
+        permute_l(1)
         flip_l(0, 1, A)
         prefetch(2)
-        permute_l(0)
-        permute_l(1)
+        spread_l(1, 1, A)
         flip_l(1, 0, A)
         prefetch(3)
         flip_l(1, 1, A)
         prefetch(4)
         multiply(0, 0)
+        spread_l(2, 0, A)
         park_l(0, A)
+        flip_l(2, 0, A)
+        spread_l(2, 1, A)
         park_l(1, A)
         for s in range(2):
             store_l(s)
         quantise(0, 0)
         multiply(0, 1)
-        spread_l(2, 0, A)
-        flip_l(2, 0, A)
-        spread_l(2, 1, A)
         for n in range(NCHIP, NB):
             if n == NSEL:
                 for s in range(2):
@@ -436,53 +478,64 @@ def tile_qriaffine_kernel(tc, layer1, layer2, layer3, h1, h2, h3, W, out):
         multiply(1, 0)
         prefetch(HBUFS + 2)
         flip_l(2, 1, A)
-        regroup_w(0, 1, A)
+        for h in range(2):
+            interleave_w(0, 0, h, A)
+        for h in range(2):
+            interleave_w(0, 1, h, A)
         quantise(0, 1)
         multiply(1, 1)
         quantise(1, 0)
-        regroup_w(0, 0, V)
-        keep_warm(0, 0, 1)
         prefetch(HBUFS + 4)
         multiply(2, 0)
-        quantise_w(0, 0)
         quantise(1, 1)
         multiply(2, 1)
+        quantise(2, 0)
         regroup_w(1, 1, A)
         regroup_w(1, 0, V)
         keep_warm(1, 0, 2)
-        quantise_w(0, 1)
+        quantise_w(0, 0)
         quantise_w(1, 0)
         for b in (0, 2):
             first_product(0, b)
             fetch_q(0, b, A)
-        quantise(2, 0)
-        quantise_w(1, 1)
-        for b in (1, 3):
-            first_product(0, b)
-            fetch_q(0, b, A)
-        due = {3: (), 4: (0,), 5: (1, 2), 6: (3,), 7: (4, 5), 8: (6,)}
-        for b in range(4):
+        quantise(2, 1)
+        quantise_w(0, 1)
+        for b in (0, 2):
             first_product(1, b)
             fetch_q(1, b, A)
+        multiply(3, 0)
+        quantise_w(1, 1)
+        for n in range(2):
+            for b in (1, 3):
+                first_product(n, b)
+                fetch_q(n, b, A)
+        due = {4: (0,), 5: (1, 2), 6: (3,), 7: (4, 5), 8: (6,)}
         for r in range(3, NB + 2):
-            if r < NB:
-                multiply(r, 0)
-            if r == 3:
-                quantise(2, 1)
-            elif r >= 5:
-                quantise(r - 2, 1)
-            if r < NB:
+            if r in PAIRS:
+                multiply_pair(r)
+            elif r < NB:
+                if r > 3:
+                    multiply(r, 0)
                 quantise(r, 0)
-            if 4 <= r <= NB:
-                multiply(r - 1, 1)
-            if r <= NB:
+                if r > 3:
+                    multiply(r - 1, 1)
+            elif r == NB:
+                quantise(NB - 2, 1)
+                multiply(NB - 1, 1)
+            else:
+                quantise(NB - 1, 1)
+            if r < NB:
                 for b in range(4):
                     first_product(r - 1, b)
                     fetch_q(r - 1, b, A)
-            for n in due.get(r, ()):
+            for i, n in enumerate(due.get(r, ())):
                 quantise_q(n)
-            for n in due.get(r, ()):
+                if r in PAIRS and i == 0:
+                    quantise_pair(r)
                 second_product(n)
-                deliver(n, A)
-        finish_half(NB - 1, 0, A)
-        finish_half(NB - 1, 1, V)
+                deliver(n, A, nc.scalar if n == NB - 2 else nc.sync)
+                if n == NB - 4:
+                    for b in range(4):
+                        first_product(NB - 1, b)
+                        fetch_q(NB - 1, b, A)
+        finish(NB - 1)

@@ -42,7 +42,7 @@ def tile_qriaffine_kernel(tc, layer1, layer2, layer3, h1, h2, h3, W, out):
 
         lr = [keep.tile([P, 512], BF16, name="lr%d" % s) for s in range(2)]
         hr = [keep.tile([P, 512], BF16, name="hr%d" % s) for s in range(2)]
-        wr = keep.tile([P, 8192], BF16, name="wr")
+        wr = [keep.tile([P, 4096], BF16, name="wr%d" % g) for g in range(2)]
         ident = keep.tile([P, P], F32, name="ident")
         identb = keep.tile([P, P], BF16, name="identb")
         selh = keep.tile([P, 2 * NSEL * P], BF16, name="selh")
@@ -50,7 +50,7 @@ def tile_qriaffine_kernel(tc, layer1, layer2, layer3, h1, h2, h3, W, out):
         hq = [keep.tile([P, 512], BF16, name="hq%d" % s) for s in range(2)]
         hh = keep.tile([P, (SLOTS - 2 * NSEL) * 1024], BF16, name="hh")
         zs = [keep.tile([P, 256], F32, name="zs%d" % s) for s in range(2)]
-        lq = [keep.tile([P, NB * P], BF16, name="lq%d" % s) for s in range(2)]
+        lq = [keep.tile([P, (NB - NPARK) * P], BF16, name="lq%d" % s) for s in range(2)]
         ys = [keep.tile([P, (NB - NPARK) * P // 2], F32, name="ys%d" % s) for s in range(2)]
         le = [keep.tile([P, NCHIP * 1024], BF16, name="le%d" % s) for s in range(2)]
         ldd = keep.tile([P, (SLOTS - 2 * NCHIP) * 1024], BF16, name="ldd")
@@ -76,14 +76,11 @@ def tile_qriaffine_kernel(tc, layer1, layer2, layer3, h1, h2, h3, W, out):
                 in_=(layer1, layer2)[s].rearrange("n (x t) a -> x n (t a)", t=2),
             )
 
-        def load_w(c8):
+        def load_w(g, c8):
             nc.sync.dma_start(
-                out=wr[c8:P:8, :].rearrange("p (b f) -> p b f", f=128),
-                in_=W[:, :, 4 * c8 : 4 * c8 + 4, :].rearrange("(i g) b j d -> i (g b) (j d)", g=2),
+                out=wr[g][c8:P:8, :].rearrange("p (b f) -> p b f", b=32),
+                in_=W[16 * g : 16 * g + 16, :, 4 * c8 : 4 * c8 + 4, :].rearrange("a b j d -> a b (j d)"),
             )
-
-        def w_rows(g, g2):
-            return wr[:, 4096 * g : 4096 * g + 4096].rearrange("p (m h j t d) -> p h t m d j", m=16, h=2, j=4, t=4, d=8)[:, g2]
 
         def constants():
             make_identity(nc, ident[:])
@@ -156,8 +153,8 @@ def tile_qriaffine_kernel(tc, layer1, layer2, layer3, h1, h2, h3, W, out):
 
         def permute_l(s):
             nc.vector.tensor_copy(
-                out=lq[s][:].bitcast(F32).rearrange("p (n i g t) -> p n i g t", i=16, g=2, t=2),
-                in_=ld[s][:].bitcast(F32).rearrange("p (n t i g) -> p n i g t", t=2, g=2, i=16),
+                out=lq[s][:].bitcast(F32).rearrange("p (n a g t) -> p n a g t", a=16, g=2, t=2),
+                in_=ld[s][:].bitcast(F32)[:, 64 * NPARK : 512].rearrange("p (n t g a) -> p n a g t", t=2, g=2, a=16),
             )
 
         def parked(s):
@@ -169,8 +166,9 @@ def tile_qriaffine_kernel(tc, layer1, layer2, layer3, h1, h2, h3, W, out):
             yps = ps_1.tile([P, 512], F32, name="acc")
             pairs = (NB - NPARK) // 2
             for q in range(pairs):
-                o = P * (q + NPARK // 2)
-                nc.tensor.transpose(yps[:, P * q : P * q + P], lq[s][:].bitcast(F32)[:, o : o + P], ident[:])
+                nc.tensor.transpose(
+                    yps[:, P * q : P * q + P], lq[s][:].bitcast(F32)[:, P * q : P * q + P], ident[:]
+                )
             copy_on(engine, ys[s][:], yps[:, 0 : P * pairs])
 
         def store_l(s):
@@ -192,27 +190,17 @@ def tile_qriaffine_kernel(tc, layer1, layer2, layer3, h1, h2, h3, W, out):
         def spread_l(n, s, engine):
             copy_on(
                 engine,
-                le[s][:].bitcast(F32)[:, 512 * n : 512 * n + 512].rearrange("p (g t i c) -> p g t i c", g=2, t=2, c=8)
-                if engine == V
-                else le[s][:].bitcast(F32)[:, 512 * n : 512 * n + 512].rearrange("p (q i c) -> p q i c", q=4, c=8),
-                ld[s][:]
-                .bitcast(F32)[:, 64 * n : 64 * n + 64]
-                .rearrange("p (t i g) -> p g t i", t=2, g=2)
-                .unsqueeze(4)
-                .to_broadcast([P, 2, 2, 16, 8])
-                if engine == V
-                else lq[s][:]
-                .bitcast(F32)[:, 64 * n : 64 * n + 64]
-                .rearrange("p (i q) -> p q i", q=4)
-                .unsqueeze(3)
-                .to_broadcast([P, 4, 16, 8]),
+                le[s][:].bitcast(F32)[:, 512 * n : 512 * n + 512].rearrange("p (k c) -> p k c", c=8),
+                ld[s][:].bitcast(F32)[:, 64 * n : 64 * n + 64].unsqueeze(2).to_broadcast([P, 64, 8]),
             )
 
         def flip_l(n, s, engine):
             lps = ps_1.tile([P, 512], F32, name="acc")
-            for q in range(4):
-                i = 512 * n + P * q
-                nc.tensor.transpose(lps[:, P * q : P * q + P], le[s][:].bitcast(F32)[:, i : i + P], ident[:])
+            for g in range(2):
+                for t in range(2):
+                    o = (2 * g + t) * P
+                    i = 512 * n + 256 * t + P * g
+                    nc.tensor.transpose(lps[:, o : o + P], le[s][:].bitcast(F32)[:, i : i + P], ident[:])
             ls = work.tile([P, 1024], BF16, name="ls", bufs=2 * NCHIP)
             copy_on(engine, ls[:].bitcast(F32), lps[:])
             live["ls", n, s] = ls
@@ -307,7 +295,7 @@ def tile_qriaffine_kernel(tc, layer1, layer2, layer3, h1, h2, h3, W, out):
             dst = wg[:, 4096 * g + 2048 * g2 : 4096 * g + 2048 * g2 + 2048].rearrange(
                 "p (t b d j) -> p t b d j", t=4, b=16, d=8, j=4
             )
-            src = w_rows(g, g2)
+            src = wr[g][:, 2048 * g2 : 2048 * g2 + 2048].rearrange("p (b j t d) -> p t b d j", b=16, j=4, t=4, d=8)
             if engine == V:
                 nc.vector.tensor_copy(out=dst[:, t0:t1], in_=src[:, t0:t1])
             else:
@@ -315,7 +303,7 @@ def tile_qriaffine_kernel(tc, layer1, layer2, layer3, h1, h2, h3, W, out):
                     nc.scalar.copy(out=dst[:, t], in_=src[:, t])
 
         def interleave_w(g, g2, h, engine):
-            src = w_rows(g, g2)
+            src = wr[g][:, 2048 * g2 : 2048 * g2 + 2048].rearrange("p (b j t d) -> p t b d j", b=16, j=4, t=4, d=8)
             wps = ps_1.tile([P, 1024], BF16, name="acc")
             for i in range(2):
                 nc.tensor.matmul(
@@ -434,14 +422,15 @@ def tile_qriaffine_kernel(tc, layer1, layer2, layer3, h1, h2, h3, W, out):
             load_l(s)
             load_h(s)
         for c8 in (0, 4, 1, 5, 2, 6, 3, 7):
-            load_w(c8)
+            load_w(0, c8)
+        for c8 in (0, 4, 1, 5, 2, 6, 3, 7):
+            load_w(1, c8)
         constants()
         selectors()
         prepare_l(0)
         permute_h(0)
         flip_h(0, A)
         spread_l(0, 0, V)
-        permute_l(0)
         flip_l(0, 0, A)
         prefetch(1)
         spread_l(1, 0, A)
@@ -449,10 +438,11 @@ def tile_qriaffine_kernel(tc, layer1, layer2, layer3, h1, h2, h3, W, out):
         permute_h(1)
         flip_h(1, A)
         spread_l(0, 1, V)
-        permute_l(1)
         flip_l(0, 1, A)
         prefetch(2)
         spread_l(1, 1, A)
+        permute_l(0)
+        permute_l(1)
         flip_l(1, 0, A)
         prefetch(3)
         flip_l(1, 1, A)

@@ -65,7 +65,7 @@ def tile_qriaffine_kernel(tc, layer1, layer2, layer3, h1, h2, h3, W, out):
             return 2 * n + 3 * s
 
         def load_h(s):
-            nc.scalar.dma_start(
+            nc.sync.dma_start(
                 out=hr[s][:].rearrange("p (n f) -> p n f", n=NB),
                 in_=(h1, h2)[s].rearrange("n (x t) a -> x n (t a)", t=2),
             )
@@ -423,8 +423,6 @@ def tile_qriaffine_kernel(tc, layer1, layer2, layer3, h1, h2, h3, W, out):
             load_h(s)
         for c8 in (0, 4, 1, 5, 2, 6, 3, 7):
             load_w(0, c8)
-        for c8 in (0, 4, 1, 5, 2, 6, 3, 7):
-            load_w(1, c8)
         constants()
         selectors()
         prepare_l(0)
@@ -441,6 +439,12 @@ def tile_qriaffine_kernel(tc, layer1, layer2, layer3, h1, h2, h3, W, out):
         flip_l(0, 1, A)
         prefetch(2)
         spread_l(1, 1, A)
+        for c8 in (0, 4, 1, 5):
+            load_w(1, c8)
+        for s in range(2):
+            park_h(s)
+        for c8 in (2, 6, 3, 7):
+            load_w(1, c8)
         permute_l(0)
         permute_l(1)
         flip_l(1, 0, A)
@@ -458,9 +462,6 @@ def tile_qriaffine_kernel(tc, layer1, layer2, layer3, h1, h2, h3, W, out):
         quantise(0, 0)
         multiply(0, 1)
         for n in range(NCHIP, NB):
-            if n == NSEL:
-                for s in range(2):
-                    park_h(s)
             for s in range(2):
                 fetch_l(s, n)
                 if n >= NSEL:

from contextlib import ExitStack

import concourse.mybir as mybir
from concourse.masks import make_identity

FLOPS = 2 * 2048 * 1024 * 1024 + 8 * 2 * 256 * 256 * 1024
BYTES = 2 * (8 * 256 * 31 * 2) + 2 * (8 * 256 * 32 * 2) + 32 * 32 * 32 * 32 * 2 + 8 * 256 * 256 * 4

BF16 = mybir.dt.bfloat16
F32 = mybir.dt.float32
U32 = mybir.dt.uint32
U8 = mybir.dt.uint8
FP8X4 = mybir.dt.float8_e4m3fn_x4
MULT = mybir.AluOpType.mult

P = 128
NB = 8
V = "vector"
A = "scalar"
NCHIP = 3
NPARK = 2
NSEL = 4
HBUFS = 4
SLOTS = 2 * NB + 2
PAIRS = (4, 5, 6)


def tile_qriaffine_kernel(tc, layer1, layer2, layer3, h1, h2, h3, W, out):
    nc = tc.nc
    with ExitStack() as ctx:
        keep = ctx.enter_context(tc.tile_pool(name="keep", bufs=1))
        work = ctx.enter_context(tc.tile_pool(name="work", bufs=3))
        ps_h = ctx.enter_context(tc.psum_pool(name="ps_h", bufs=HBUFS))
        ps_1 = ctx.enter_context(tc.psum_pool(name="ps_1", bufs=8 - HBUFS))
        ctx.enter_context(tc.manual_schedule())

        def copy_on(engine, dst, src):
            if engine == V:
                nc.vector.tensor_copy(out=dst, in_=src)
            else:
                nc.scalar.copy(out=dst, in_=src)

        lr = [keep.tile([P, 512], BF16, name="lr%d" % s) for s in range(2)]
        hr = [keep.tile([P, 512], BF16, name="hr%d" % s) for s in range(2)]
        wr = [keep.tile([P, 4096], BF16, name="wr%d" % g) for g in range(2)]
        ident = keep.tile([P, P], F32, name="ident")
        identb = keep.tile([P, P], BF16, name="identb")
        selh = keep.tile([P, 2 * NSEL * P], BF16, name="selh")
        ld = [keep.tile([P, 1024], BF16, name="ld%d" % s) for s in range(2)]
        hq = [keep.tile([P, 512], BF16, name="hq%d" % s) for s in range(2)]
        hh = keep.tile([P, (SLOTS - 2 * NSEL) * 1024], BF16, name="hh")
        zs = [keep.tile([P, 256], F32, name="zs%d" % s) for s in range(2)]
        lq = [keep.tile([P, (NB - NPARK) * P], BF16, name="lq%d" % s) for s in range(2)]
        ys = [keep.tile([P, (NB - NPARK) * P // 2], F32, name="ys%d" % s) for s in range(2)]
        le = [keep.tile([P, NCHIP * 1024], BF16, name="le%d" % s) for s in range(2)]
        ldd = keep.tile([P, (SLOTS - 2 * NCHIP) * 1024], BF16, name="ldd")
        codes = keep.tile([P, SLOTS * 512], U32, name="codes", align_bytes=64)
        planes = keep.tile([P, SLOTS * 512], U8, name="planes", align_bytes=64)
        wg = keep.tile([P, 8192], BF16, name="wg", align_bytes=64)
        wc = keep.tile([P, 2048], U32, name="wc", align_bytes=64)
        ws = keep.tile([P, 2048], U8, name="ws", align_bytes=64)
        live = {}

        def slot(n, s):
            return 2 * n + 3 * s

        def load_h(s):
            nc.sync.dma_start(
                out=hr[s][:].rearrange("p (n f) -> p n f", n=NB),
                in_=(h1, h2)[s].rearrange("n (x t) a -> x n (t a)", t=2),
            )

        def load_l(s):
            nc.sync.dma_start(
                out=lr[s][:].rearrange("p (n f) -> p n f", n=NB)[:, :, 0:62],
                in_=(layer1, layer2)[s].rearrange("n (x t) a -> x n (t a)", t=2),
            )

        def load_w(g, c8):
            nc.sync.dma_start(
                out=wr[g][c8:P:8, :].rearrange("p (b f) -> p b f", b=32),
                in_=W[16 * g : 16 * g + 16, :, 4 * c8 : 4 * c8 + 4, :].rearrange("a b j d -> a b (j d)"),
            )

        def constants():
            make_identity(nc, ident[:])
            for s in range(2):
                nc.vector.memset(ld[s][:].rearrange("p (q a e) -> p q a e", a=32, e=2)[:, :, 31, :], 1.0)

        def selectors():
            nc.vector.tensor_copy(out=identb[:], in_=ident[:])
            for t in range(2):
                nc.vector.tensor_copy(
                    out=selh[:].rearrange("p (n t a c) -> p t n a c", t=2, a=16, c=8)[:, t],
                    in_=identb[:]
                    .rearrange("p (n c t) -> p t n c", c=8, t=2)[:, t, 0:NSEL]
                    .unsqueeze(2)
                    .to_broadcast([P, NSEL, 16, 8]),
                )

        def permute_h(s):
            if s == 0:
                nc.vector.tensor_copy(
                    out=hq[0][:].bitcast(F32).rearrange("p (u n c t) -> p u n c t", u=2, c=8, t=2),
                    in_=hr[0][:].bitcast(F32).rearrange("p (n t c u) -> p u n c t", u=2, c=8, t=2),
                )
                return
            for u in range(2):
                nc.vector.tensor_copy(
                    out=hq[1][:].rearrange("p (u n d t e) -> p u n d t e", u=2, d=8, t=2, e=2)[:, u],
                    in_=hr[1][:].rearrange("p (n t u e d) -> p u n d t e", u=2, e=2, d=8, t=2)[:, u],
                )

        def flip_h(s, engine):
            zps = ps_1.tile([P, 512], F32, name="acc")
            for u in range(2):
                nc.tensor.transpose(
                    zps[:, P * u : P * u + P], hq[s][:].bitcast(F32)[:, P * u : P * u + P], ident[:]
                )
            copy_on(
                engine,
                zs[s][:].rearrange("p (x u) -> p x u", u=2),
                zps[:, 0:256].rearrange("p (u x) -> p x u", u=2),
            )

        def h_parked(s):
            words = (NB - NSEL) * 16 * 256
            base = NB * 65536 - 2 * (NB - NPARK) * 64 * P - (2 - s) * words
            return out.rearrange("n i j -> (n i j)")[base : base + words]

        def park_h(s):
            nc.sync.dma_start(out=h_parked(s).rearrange("(m w) -> m w", w=256), in_=zs[s][16 * NSEL : P, :])

        def fetch_h(s, n):
            base = (n - NSEL) * 16 * 256
            nc.sync.dma_start(
                out=hh[:].bitcast(F32)[:, 512 * (slot(n, s) - 2 * NSEL) : 512 * (slot(n, s) - 2 * NSEL) + 512],
                in_=h_parked(s)[base : base + 16 * 256]
                .rearrange("(c f) -> c f", f=512)
                .unsqueeze(0)
                .to_broadcast([16, 8, 512]),
            )

        def prepare_l(s):
            nc.vector.tensor_copy(
                out=ld[s][:].rearrange("p (n t a e) -> p n t a e", t=2, a=32, e=2)[:, :, :, 0:31, :],
                in_=lr[s][:]
                .rearrange("p (n f) -> p n f", n=NB)[:, :, 0:62]
                .rearrange("p n (t a) -> p n t a", t=2)
                .unsqueeze(4)
                .to_broadcast([P, NB, 2, 31, 2]),
            )

        def permute_l(s):
            nc.vector.tensor_copy(
                out=lq[s][:].bitcast(F32).rearrange("p (n a g t) -> p n a g t", a=16, g=2, t=2),
                in_=ld[s][:].bitcast(F32)[:, 64 * NPARK : 512].rearrange("p (n t g a) -> p n a g t", t=2, g=2, a=16),
            )

        def parked(s):
            words = (NB - NPARK) * 64 * P
            base = NB * 65536 - (2 - s) * words
            return out.rearrange("n i j -> (n i j)")[base : base + words]

        def park_l(s, engine):
            yps = ps_1.tile([P, 512], F32, name="acc")
            pairs = (NB - NPARK) // 2
            for q in range(pairs):
                nc.tensor.transpose(
                    yps[:, P * q : P * q + P], lq[s][:].bitcast(F32)[:, P * q : P * q + P], ident[:]
                )
            copy_on(engine, ys[s][:], yps[:, 0 : P * pairs])

        def store_l(s):
            nc.sync.dma_start(
                out=parked(s).rearrange("(q m x) -> m q x", m=P, x=P),
                in_=ys[s][:].rearrange("p (q x) -> p q x", x=P),
            )

        def fetch_l(s, n):
            base = (n - NPARK) * 64 * P
            nc.sync.dma_start(
                out=ldd[:].bitcast(F32)[:, 512 * (slot(n, s) - 2 * NCHIP) : 512 * (slot(n, s) - 2 * NCHIP) + 512],
                in_=parked(s)[base : base + 64 * P]
                .rearrange("(a f) -> a f", f=512)
                .unsqueeze(1)
                .to_broadcast([16, 8, 512]),
            )

        def spread_l(n, s, engine):
            copy_on(
                engine,
                le[s][:].bitcast(F32)[:, 512 * n : 512 * n + 512].rearrange("p (k c) -> p k c", c=8),
                ld[s][:].bitcast(F32)[:, 64 * n : 64 * n + 64].unsqueeze(2).to_broadcast([P, 64, 8]),
            )

        def flip_l(n, s, engine):
            lps = ps_1.tile([P, 512], F32, name="acc")
            for g in range(2):
                for t in range(2):
                    o = (2 * g + t) * P
                    i = 512 * n + 256 * t + P * g
                    nc.tensor.transpose(lps[:, o : o + P], le[s][:].bitcast(F32)[:, i : i + P], ident[:])
            ls = work.tile([P, 1024], BF16, name="ls", bufs=2 * NCHIP)
            copy_on(engine, ls[:].bitcast(F32), lps[:])
            live["ls", n, s] = ls

        def select_h(n, s):
            hps = ps_h.tile([P, 1024], BF16, name="hps")
            for t in range(2):
                k = 2 * n + t
                nc.tensor.matmul(
                    out=hps[:, 512 * t : 512 * t + 512],
                    lhsT=selh[:, P * k : P * k + P],
                    rhs=zs[s][:].bitcast(BF16),
                    start=True,
                    stop=True,
                )
            live["hps", n, s] = hps

        def room(n, s):
            if n + s not in PAIRS:
                if ("grouped", n, s) not in live:
                    grouped = work.tile([P, 2048], BF16, name="grouped", align_bytes=64)
                    live["grouped", n, s] = grouped
                return live["grouped", n, s][:]
            if ("pair", n + s) not in live:
                pair = work.tile([P, 4096], BF16, name="pair", align_bytes=64, bufs=2)
                live["pair", n + s] = pair
            return live["pair", n + s][:, 2048 * s : 2048 * s + 2048]

        def l_source(n, s):
            if n < NCHIP:
                return live["ls", n, s][:]
            o = 1024 * (slot(n, s) - 2 * NCHIP)
            return ldd[:, o : o + 1024]

        def h_source(n, s):
            if n < NSEL:
                return live["hps", n, s][:]
            o = 1024 * (slot(n, s) - 2 * NSEL)
            return hh[:, o : o + 1024]

        def multiply(n, s):
            nc.vector.tensor_tensor(
                out=room(n, s).rearrange("p (g w u e) -> p g w u e", g=2, u=2, e=2),
                in0=h_source(n, s)
                .rearrange("p (w u e) -> p w u e", u=2, e=2)
                .unsqueeze(1)
                .to_broadcast([P, 2, 256, 2, 2]),
                in1=l_source(n, s)
                .rearrange("p (g w e) -> p g w e", g=2, e=2)
                .unsqueeze(3)
                .to_broadcast([P, 2, 256, 2, 2]),
                op=MULT,
            )

        def multiply_pair(m):
            if m - 1 < NSEL:
                multiply(m, 0)
                multiply(m - 1, 1)
                return
            room(m, 0)
            ho = 1024 * (slot(m, 0) - 2 * NSEL)
            lo = 1024 * (slot(m, 0) - 2 * NCHIP)
            nc.vector.tensor_tensor(
                out=live["pair", m][:].rearrange("p (s g f) -> p s g f", s=2, g=2),
                in0=hh[:, ho : ho + 2048]
                .rearrange("p (s f) -> p s f", s=2)
                .unsqueeze(2)
                .to_broadcast([P, 2, 2, 1024]),
                in1=ldd[:, lo : lo + 2048]
                .rearrange("p (w e) -> p w e", e=2)
                .unsqueeze(2)
                .to_broadcast([P, 1024, 2, 2]),
                op=MULT,
            )

        def quantise_slots(first, count, source):
            o = 512 * first
            w = 512 * count
            nc.vector.quantize_mx(
                out=codes[:, o : o + w].bitcast(FP8X4),
                scales=planes[:, o : o + w],
                in_=source,
            )

        def quantise(n, s):
            quantise_slots(slot(n, s), 1, room(n, s))

        def quantise_pair(m):
            quantise_slots(slot(m, 0), 2, live["pair", m][:])

        def regroup_w(g, g2, engine, t0=0, t1=4):
            dst = wg[:, 4096 * g + 2048 * g2 : 4096 * g + 2048 * g2 + 2048].rearrange(
                "p (t b d j) -> p t b d j", t=4, b=16, d=8, j=4
            )
            src = wr[g][:, 2048 * g2 : 2048 * g2 + 2048].rearrange("p (b j t d) -> p t b d j", b=16, j=4, t=4, d=8)
            if engine == V:
                nc.vector.tensor_copy(out=dst[:, t0:t1], in_=src[:, t0:t1])
            else:
                for t in range(t0, t1):
                    nc.scalar.copy(out=dst[:, t], in_=src[:, t])

        def interleave_w(g, g2, h, engine):
            src = wr[g][:, 2048 * g2 : 2048 * g2 + 2048].rearrange("p (b j t d) -> p t b d j", b=16, j=4, t=4, d=8)
            wps = ps_1.tile([P, 1024], BF16, name="acc")
            for i in range(2):
                nc.tensor.matmul(
                    out=wps[:, 512 * i : 512 * i + 512], lhsT=identb[:], rhs=src[:, 2 * h + i], start=True, stop=True
                )
            o = 4096 * g + 2048 * g2 + 1024 * h
            copy_on(engine, wg[:, o : o + 1024], wps[:])

        def keep_warm(g, g2, times):
            for i in range(times):
                idle = ps_1.tile([P, 512], F32, name="acc")
                o = 4096 * g + 2048 * g2 + 512 * i
                nc.tensor.matmul(out=idle[:], lhsT=identb[:], rhs=wg[:, o : o + 512], start=True, stop=True)

        def quantise_w(g, g2):
            o = 1024 * g + 512 * g2
            nc.vector.quantize_mx(
                out=wc[:, o : o + 512].bitcast(FP8X4),
                scales=ws[:, o : o + 512],
                in_=wg[:, 4 * o : 4 * o + 2048],
            )

        def first_product(n, b):
            t, g2 = divmod(b, 2)
            acc = ps_1.tile([P, 512], F32, name="acc")
            for tt in range(4):
                for g in range(2):
                    wo = 1024 * g + 512 * g2 + P * tt
                    po = 512 * slot(n, 0) + 256 * g + P * t
                    nc.tensor.matmul_mx(
                        out=acc[:, P * tt : P * tt + P],
                        lhsT=wc[:, wo : wo + P].bitcast(FP8X4),
                        lhsT_scale=ws[:, wo : wo + P],
                        rhs=codes[:, po : po + P].bitcast(FP8X4),
                        rhs_scale=planes[:, po : po + P],
                        start=(g == 0),
                        stop=(g == 1),
                    )
            live["acc", n, b] = acc

        def fetch_q(n, b, engine):
            if ("qg", n) not in live:
                qg = work.tile([P, 2048], BF16, name="qg", align_bytes=64)
                live["qg", n] = qg
            copy_on(
                engine,
                live["qg", n][:, 512 * b : 512 * b + 512].rearrange("p (w k) -> p w k", k=4),
                live["acc", n, b][:].rearrange("p (k w) -> p w k", k=4),
            )

        def quantise_q(n, halves=(0, 1)):
            if ("qc", n) not in live:
                qc = work.tile([P, 512], U32, name="qc", align_bytes=64)
                qs = work.tile([P, 512], U8, name="qs", align_bytes=64)
                live["qc", n] = qc
                live["qs", n] = qs
            lo, hi = 256 * halves[0], 256 * halves[-1] + 256
            nc.vector.quantize_mx(
                out=live["qc", n][:, lo:hi].bitcast(FP8X4),
                scales=live["qs", n][:, lo:hi],
                in_=live["qg", n][:, 4 * lo : 4 * hi],
            )

        def second_passes(n, t, dst):
            for g2 in range(2):
                qo = 256 * t + P * g2
                ro = 512 * slot(n, 1) + 256 * g2
                nc.tensor.matmul_mx(
                    out=dst,
                    lhsT=live["qc", n][:, qo : qo + P].bitcast(FP8X4),
                    lhsT_scale=live["qs", n][:, qo : qo + P],
                    rhs=codes[:, ro : ro + 256].bitcast(FP8X4),
                    rhs_scale=planes[:, ro : ro + 256],
                    start=(g2 == 0),
                    stop=(g2 == 1),
                )

        def second_product(n):
            res = ps_1.tile([P, 512], F32, name="acc")
            for t in range(2):
                second_passes(n, t, res[:, 256 * t : 256 * t + 256])
            live["res", n] = res

        def finish(n):
            for t in range(2):
                quantise_q(n, (t,))
            for t in range(2):
                res = ps_1.tile([P, 512], F32, name="acc")
                second_passes(n, t, res[:, 0:256])
                ob = work.tile([P, 512], F32, name="ob", bufs=6)
                nc.vector.tensor_copy(
                    out=ob[:, 0:256].rearrange("p (x s) -> p x s", s=2),
                    in_=res[:, 0:256].rearrange("p (s x) -> p x s", s=2),
                )
                nc.sync.dma_start(out=out[n].rearrange("(x t) j -> x t j", t=2)[:, t, :], in_=ob[:, 0:256])

        def deliver(n, engine, queue):
            ob = work.tile([P, 512], F32, name="ob", bufs=6)
            copy_on(
                engine,
                ob[:].rearrange("p (t x s) -> p t x s", t=2, s=2),
                live["res", n][:].rearrange("p (t s x) -> p t x s", t=2, s=2),
            )
            queue.dma_start(out=out[n].rearrange("(x t) j -> x (t j)", t=2), in_=ob[:])

        order = [(n, s) for n in range(NSEL) for s in range(2)]
        selected = []

        def prefetch(limit):
            while len(selected) < min(limit, len(order)):
                n, s = order[len(selected)]
                select_h(n, s)
                selected.append((n, s))

        for s in range(2):
            load_l(s)
            load_h(s)
        for c8 in (0, 4, 1, 5, 2, 6, 3, 7):
            load_w(0, c8)
        constants()
        selectors()
        prepare_l(0)
        permute_h(0)
        flip_h(0, A)
        spread_l(0, 0, V)
        flip_l(0, 0, A)
        prefetch(1)
        spread_l(1, 0, A)
        prepare_l(1)
        permute_h(1)
        flip_h(1, A)
        spread_l(0, 1, V)
        flip_l(0, 1, A)
        prefetch(2)
        spread_l(1, 1, A)
        for c8 in (0, 4, 1, 5):
            load_w(1, c8)
        for s in range(2):
            park_h(s)
        for c8 in (2, 6, 3, 7):
            load_w(1, c8)
        permute_l(0)
        permute_l(1)
        flip_l(1, 0, A)
        prefetch(3)
        flip_l(1, 1, A)
        prefetch(4)
        multiply(0, 0)
        spread_l(2, 0, A)
        park_l(0, A)
        flip_l(2, 0, A)
        spread_l(2, 1, A)
        park_l(1, A)
        for s in range(2):
            store_l(s)
        quantise(0, 0)
        multiply(0, 1)
        for n in range(NCHIP, NB):
            for s in range(2):
                fetch_l(s, n)
                if n >= NSEL:
                    fetch_h(s, n)
        multiply(1, 0)
        prefetch(HBUFS + 2)
        flip_l(2, 1, A)
        for h in range(2):
            interleave_w(0, 0, h, A)
        for h in range(2):
            interleave_w(0, 1, h, A)
        quantise(0, 1)
        multiply(1, 1)
        quantise(1, 0)
        prefetch(HBUFS + 4)
        multiply(2, 0)
        quantise(1, 1)
        multiply(2, 1)
        quantise(2, 0)
        regroup_w(1, 1, A)
        regroup_w(1, 0, V)
        keep_warm(1, 0, 2)
        quantise_w(0, 0)
        quantise_w(1, 0)
        for b in (0, 2):
            first_product(0, b)
            fetch_q(0, b, A)
        quantise(2, 1)
        quantise_w(0, 1)
        for b in (0, 2):
            first_product(1, b)
            fetch_q(1, b, A)
        multiply(3, 0)
        quantise_w(1, 1)
        for n in range(2):
            for b in (1, 3):
                first_product(n, b)
                fetch_q(n, b, A)
        due = {4: (0,), 5: (1, 2), 6: (3,), 7: (4, 5), 8: (6,)}
        for r in range(3, NB + 2):
            if r in PAIRS:
                multiply_pair(r)
            elif r < NB:
                if r > 3:
                    multiply(r, 0)
                quantise(r, 0)
                if r > 3:
                    multiply(r - 1, 1)
            elif r == NB:
                quantise(NB - 2, 1)
                multiply(NB - 1, 1)
            else:
                quantise(NB - 1, 1)
            if r < NB:
                for b in range(4):
                    first_product(r - 1, b)
                    fetch_q(r - 1, b, A)
            for i, n in enumerate(due.get(r, ())):
                quantise_q(n)
                if r in PAIRS and i == 0:
                    quantise_pair(r)
                second_product(n)
                deliver(n, A, nc.scalar if n == NB - 2 else nc.sync)
                if n == NB - 4:
                    for b in range(4):
                        first_product(NB - 1, b)
                        fetch_q(NB - 1, b, A)
        finish(NB - 1)
